import numpy as np
import ml_dtypes

BF16 = ml_dtypes.bfloat16


def bf(x):
    return np.asarray(x, np.float32).astype(BF16)


def f32(x):
    return np.asarray(x, np.float32)


def f64(x):
    return np.asarray(x).astype(np.float64)


def striped(idx):
    return np.tile(idx.reshape(-1, 16).T, (8, 1))


C, F, S, N = 256, 512, 2048, 512
EPS = 1e-8
ALPHA = 1.702


def setup_inputs():
    base = f32(np.random.standard_normal((C, S)))
    x = f32((0.5 + np.random.rand(1, N)) * np.random.standard_normal((C, N)) + 0.5 * np.random.standard_normal((1, N)))
    gain = f32(1.0 + 0.1 * np.random.standard_normal((C, 1)))
    shift = f32(0.1 * np.random.standard_normal((C, 1)))
    w1 = bf(np.concatenate([np.random.standard_normal((C, F)), 0.25 * np.random.standard_normal((C, F))], axis=1) / np.sqrt(C))
    w2 = bf(np.random.standard_normal((F + F, C)) / np.sqrt(F))
    return {"base": base, "x": x, "gain": gain, "shift": shift, "w1": w1, "w2": w2, "offs": striped(np.random.permutation(S)[:N])}


def reference(base, x, gain, shift, w1, w2, offs):
    idx = offs[:16].T.reshape(-1)
    x = f64(x)
    xc = x - x.mean(axis=0, keepdims=True)
    var = (xc**2).mean(axis=0, keepdims=True)
    xn = f64(gain) * (xc / np.sqrt(var + EPS)) + f64(shift)
    h = f64(w1).T @ xn
    p, q = h[:F], h[F:]
    e = np.exp(-ALPHA * p)
    u = 1.0 + e * np.cos(ALPHA * q)
    v = e * np.sin(ALPHA * q)
    d = u**2 + v**2
    ar = (p * u - q * v) / d
    ai = (p * v + q * u) / d
    hid = np.concatenate([ar, -ai], axis=0)
    out = f64(base).copy()
    out[:, idx] = f64(w2).T @ hid + x
    return out

@@ -1,0 +1,194 @@
+import math
+
+import concourse.mybir as mybir
+from concourse.masks import make_identity
+
+FP32 = mybir.dt.float32
+BF16 = mybir.dt.bfloat16
+U16 = mybir.dt.uint16
+I32 = mybir.dt.int32
+ALU = mybir.AluOpType
+ACT = mybir.ActivationFunctionType
+
+P = 128
+C, F, S, N = 256, 512, 2048, 512
+CB = C // P
+FB = F // P
+EPS = 1e-8
+ALPHA = 1.702
+
+FLOPS = 2 * C * (2 * F) * N + 2 * (2 * F) * C * N
+
+TURNS_PER_Q = ALPHA / (2.0 * math.pi)
+TWO_PI_BELOW = 6.2831850051879883
+
+E_CAP = 2.0**31
+
+
+def tile_retnetclm_kernel(tc, base, x, gain, shift, w1, w2, offs, out):
+    nc = tc.nc
+    with (
+        tc.tile_pool(name="held", bufs=1) as held,
+        tc.tile_pool(name="work", bufs=2) as work,
+        tc.psum_pool(name="banks", bufs=8) as banks,
+    ):
+        x_sb = [held.tile([P, N], FP32, name=f"x_sb{cb}") for cb in range(CB)]
+        nc.sync.dma_start(x_sb[0][:], x[0:P, :])
+        nc.scalar.dma_start(x_sb[1][:], x[P : 2 * P, :])
+
+        offsets = held.tile([P, N // 16], U16, name="offsets")
+        nc.sync.dma_start(offsets[:], offs)
+
+        rows = held.tile([64, P], FP32, name="rows")
+        nc.gpsimd.memset(rows[:], 0.0)
+        nc.sync.dma_start(rows[0:CB, :], gain.rearrange("(b p) o -> b (p o)", p=P))
+        nc.scalar.dma_start(rows[CB : 2 * CB, :], shift.rearrange("(b p) o -> b (p o)", p=P))
+
+        w1_sb = [held.tile([P, 2 * F], BF16, name=f"w1_sb{cb}") for cb in range(CB)]
+        nc.sync.dma_start(w1_sb[0][:], w1[0:P, :])
+        nc.scalar.dma_start(w1_sb[1][:], w1[P : 2 * P, :])
+        w2_sb = held.tile([P, 2 * FB, C], BF16, name="w2_sb")
+        nc.sync.dma_start(w2_sb[:], w2.rearrange("(k p) c -> p k c", p=P))
+
+        window = [held.tile([P, S], FP32, name=f"window{cb}") for cb in range(CB)]
+        nc.sync.dma_start(window[0][:], base[0:P, :])
+        nc.scalar.dma_start(window[1][:], base[P : 2 * P, :])
+
+        mean_weights = held.tile([P, P], FP32, name="mean_weights")
+        nc.vector.memset(mean_weights[:], 1.0 / C)
+        identity = held.tile([64, 64], FP32, name="identity")
+        make_identity(nc, identity[:])
+
+        mean_ps = banks.tile([P, N], FP32, name="mean_ps", tag="bank")
+        for cb in range(CB):
+            nc.tensor.matmul(
+                mean_ps[:], mean_weights[:], x_sb[cb][:], start=(cb == 0), stop=(cb == CB - 1)
+            )
+        centred = [held.tile([P, N], FP32, name=f"centred{cb}") for cb in range(CB)]
+        squared = [held.tile([P, N], FP32, name=f"squared{cb}") for cb in range(CB)]
+        var_ps = banks.tile([P, N], FP32, name="var_ps", tag="bank")
+        for cb in range(CB):
+            nc.vector.tensor_tensor(centred[cb][:], x_sb[cb][:], mean_ps[:], ALU.subtract)
+            nc.vector.tensor_tensor(squared[cb][:], centred[cb][:], centred[cb][:], ALU.mult)
+            nc.tensor.matmul(
+                var_ps[:], mean_weights[:], squared[cb][:], start=(cb == 0), stop=(cb == CB - 1)
+            )
+        columns_ps = banks.tile([P, 64], FP32, name="columns_ps", tag="bank")
+        nc.tensor.transpose(columns_ps[:], rows[:], identity[:])
+        columns = held.tile([P, 2 * CB], FP32, name="columns")
+        nc.vector.tensor_copy(columns[:], columns_ps[:, 0 : 2 * CB])
+
+        ln_var = held.tile([P, N], FP32, name="ln_var")
+        nc.scalar.activation(ln_var[:], var_ps[:], ACT.Ln, bias=EPS)
+        rstd = held.tile([P, N], FP32, name="rstd")
+        nc.scalar.activation(rstd[:], ln_var[:], ACT.Exp, scale=-0.5)
+
+        xn = [held.tile([P, N], BF16, name=f"xn{cb}") for cb in range(CB)]
+        for cb in range(CB):
+            scaled = held.tile([P, N], FP32, name=f"scaled{cb}")
+            nc.vector.tensor_tensor(scaled[:], centred[cb][:], rstd[:], ALU.mult)
+            nc.scalar.activation(
+                xn[cb][:],
+                scaled[:],
+                ACT.Identity,
+                scale=columns[:, cb : cb + 1],
+                bias=columns[:, CB + cb : CB + cb + 1],
+            )
+
+
+        p_ps, q_ps, e_twice, e_squared, turn_part = [], [], [], [], []
+        for fb in range(FB):
+            p_ps.append(banks.tile([P, N], FP32, name="p_ps", tag="bank"))
+            q_ps.append(banks.tile([P, N], FP32, name="q_ps", tag="bank"))
+            for h_ps, first_column in ((p_ps[fb], fb * P), (q_ps[fb], F + fb * P)):
+                for cb in range(CB):
+                    nc.tensor.matmul(
+                        h_ps[:],
+                        w1_sb[cb][:, first_column : first_column + P],
+                        xn[cb][:],
+                        start=(cb == 0),
+                        stop=(cb == CB - 1),
+                    )
+            e_twice.append(work.tile([P, N], FP32, name="e_twice", bufs=FB))
+            nc.scalar.activation(e_twice[fb][:], p_ps[fb][:], ACT.Exp, scale=-ALPHA, bias=math.log(2.0))
+            e_squared.append(work.tile([P, N], FP32, name="e_squared", bufs=FB))
+            nc.scalar.activation(e_squared[fb][:], p_ps[fb][:], ACT.Exp, scale=-2.0 * ALPHA)
+
+            whole_turns = work.tile([P, N], I32, name="whole_turns")
+            nc.vector.tensor_scalar(whole_turns[:], q_ps[fb][:], TURNS_PER_Q, None, ALU.mult)
+            turn_part.append(work.tile([P, N], FP32, name="turn_part", bufs=FB))
+            nc.vector.scalar_tensor_tensor(
+                turn_part[fb][:], q_ps[fb][:], TURNS_PER_Q, whole_turns[:], ALU.mult, ALU.subtract
+            )
+
+        d_minus_1, twice_num_re, twice_num_im_neg = [], [], []
+        for fb in range(FB):
+            sine = work.tile([P, N], FP32, name="sine")
+            nc.scalar.activation(sine[:], turn_part[fb][:], ACT.Sin, scale=TWO_PI_BELOW)
+            turn_part_abs = work.tile([P, N], FP32, name="turn_part_abs")
+            nc.scalar.activation(turn_part_abs[:], turn_part[fb][:], ACT.Abs)
+            cosine = work.tile([P, N], FP32, name="cosine")
+            nc.scalar.activation(
+                cosine[:], turn_part_abs[:], ACT.Sin, scale=-TWO_PI_BELOW, bias=math.pi / 2.0
+            )
+
+            x2 = work.tile([P, N], FP32, name="x2")
+            nc.vector.scalar_tensor_tensor(
+                x2[:], e_twice[fb][:], 2.0 * E_CAP, cosine[:], ALU.min, ALU.mult
+            )
+            y2 = work.tile([P, N], FP32, name="y2")
+            nc.vector.scalar_tensor_tensor(
+                y2[:], e_twice[fb][:], 2.0 * E_CAP, sine[:], ALU.min, ALU.mult
+            )
+            d_minus_1.append(work.tile([P, N], FP32, name="d_minus_1", bufs=FB))
+            nc.vector.scalar_tensor_tensor(
+                d_minus_1[fb][:], e_squared[fb][:], E_CAP * E_CAP, x2[:], ALU.min, ALU.add
+            )
+
+            u2_p = work.tile([P, N], FP32, name="u2_p")
+            nc.vector.scalar_tensor_tensor(u2_p[:], x2[:], 2.0, p_ps[fb][:], ALU.add, ALU.mult)
+            y2_q = work.tile([P, N], FP32, name="y2_q")
+            nc.vector.tensor_tensor(y2_q[:], y2[:], q_ps[fb][:], ALU.mult)
+            twice_num_re.append(work.tile([P, N], FP32, name="twice_num_re", bufs=FB))
+            nc.vector.tensor_tensor(twice_num_re[fb][:], u2_p[:], y2_q[:], ALU.subtract)
+
+            y2_p = work.tile([P, N], FP32, name="y2_p")
+            nc.vector.tensor_tensor(y2_p[:], y2[:], p_ps[fb][:], ALU.mult)
+            u2_q = work.tile([P, N], FP32, name="u2_q")
+            nc.vector.scalar_tensor_tensor(u2_q[:], x2[:], 2.0, q_ps[fb][:], ALU.add, ALU.mult)
+            twice_num_im_neg.append(work.tile([P, N], FP32, name="twice_num_im_neg", bufs=FB))
+            nc.vector.scalar_tensor_tensor(
+                twice_num_im_neg[fb][:], y2_p[:], -1.0, u2_q[:], ALU.mult, ALU.subtract
+            )
+
+        ln_d = []
+        for fb in range(FB):
+            ln_d.append(work.tile([P, N], FP32, name="ln_d", bufs=FB))
+            nc.scalar.activation(ln_d[fb][:], d_minus_1[fb][:], ACT.Ln, bias=1.0)
+
+        y_ps = [banks.tile([P, N], FP32, name=f"y_ps{cb}", tag="bank") for cb in range(CB)]
+        for fb in range(FB):
+            half_over_d = work.tile([P, N], FP32, name="half_over_d")
+            nc.scalar.activation(
+                half_over_d[:], ln_d[fb][:], ACT.Exp, scale=-1.0, bias=-math.log(2.0)
+            )
+            a_re = work.tile([P, N], BF16, name="a_re")
+            nc.vector.tensor_tensor(a_re[:], twice_num_re[fb][:], half_over_d[:], ALU.mult)
+            a_im_neg = work.tile([P, N], BF16, name="a_im_neg")
+            nc.vector.tensor_tensor(a_im_neg[:], twice_num_im_neg[fb][:], half_over_d[:], ALU.mult)
+            for cb in range(CB):
+                channels = slice(cb * P, (cb + 1) * P)
+                nc.tensor.matmul(
+                    y_ps[cb][:], w2_sb[:, fb, channels], a_re[:], start=(fb == 0), stop=False
+                )
+                nc.tensor.matmul(
+                    y_ps[cb][:], w2_sb[:, FB + fb, channels], a_im_neg[:], start=False, stop=(fb == FB - 1)
+                )
+
+        for cb in range(CB):
+            y_sb = held.tile([P, N], FP32, name=f"y_sb{cb}")
+            nc.scalar.copy(y_sb[:], y_ps[cb][:])
+            nc.vector.tensor_tensor(
+                window[cb][:].indirect(offsets[:]), y_sb[:], x_sb[cb][:], ALU.add
+            )
+            nc.sync.dma_start(out[cb * P : (cb + 1) * P, :], window[cb][:])

@@ -59,41 +59,59 @@ def tile_retnetclm_kernel(tc, base, x, gain, shift, w1, w2, offs, out):
         identity = held.tile([64, 64], FP32, name="identity")
         make_identity(nc, identity[:])
 
-        mean_ps = banks.tile([P, N], FP32, name="mean_ps", tag="bank")
-        for cb in range(CB):
+        half_columns = [slice(half * (N // 2), (half + 1) * (N // 2)) for half in range(2)]
+        x_sum = held.tile([P, N], FP32, name="x_sum")
+        mean_ps = []
+        for columns_of_half in half_columns:
+            nc.vector.tensor_tensor(
+                x_sum[:, columns_of_half], x_sb[0][:, columns_of_half], x_sb[1][:, columns_of_half], ALU.add
+            )
+            mean_ps.append(banks.tile([P, N // 2], FP32, name="mean_ps", tag="bank"))
             nc.tensor.matmul(
-                mean_ps[:], mean_weights[:], x_sb[cb][:], start=(cb == 0), stop=(cb == CB - 1)
+                mean_ps[-1][:], mean_weights[:], x_sum[:, columns_of_half], start=True, stop=True
             )
         centred = [held.tile([P, N], FP32, name=f"centred{cb}") for cb in range(CB)]
         squared = [held.tile([P, N], FP32, name=f"squared{cb}") for cb in range(CB)]
-        var_ps = banks.tile([P, N], FP32, name="var_ps", tag="bank")
-        for cb in range(CB):
-            nc.vector.tensor_tensor(centred[cb][:], x_sb[cb][:], mean_ps[:], ALU.subtract)
-            nc.vector.tensor_tensor(squared[cb][:], centred[cb][:], centred[cb][:], ALU.mult)
-            nc.tensor.matmul(
-                var_ps[:], mean_weights[:], squared[cb][:], start=(cb == 0), stop=(cb == CB - 1)
+        squared_sum = held.tile([P, N], FP32, name="squared_sum")
+        rstd = held.tile([P, N], FP32, name="rstd")
+        for half, columns_of_half in enumerate(half_columns):
+            for cb in range(CB):
+                nc.vector.tensor_tensor(
+                    centred[cb][:, columns_of_half], x_sb[cb][:, columns_of_half], mean_ps[half][:], ALU.subtract
+                )
+            for cb in range(CB):
+                nc.vector.tensor_tensor(
+                    squared[cb][:, columns_of_half],
+                    centred[cb][:, columns_of_half],
+                    centred[cb][:, columns_of_half],
+                    ALU.mult,
+                )
+            nc.vector.tensor_tensor(
+                squared_sum[:, columns_of_half],
+                squared[0][:, columns_of_half],
+                squared[1][:, columns_of_half],
+                ALU.add,
             )
+            var_ps = banks.tile([P, N // 2], FP32, name="var_ps", tag="bank")
+            nc.tensor.matmul(
+                var_ps[:], mean_weights[:], squared_sum[:, columns_of_half], start=True, stop=True
+            )
+            nc.scalar.activation(
+                rstd[:, columns_of_half], var_ps[:], ACT.Abs_reciprocal_sqrt, bias=EPS
+            )
+
         columns_ps = banks.tile([P, 64], FP32, name="columns_ps", tag="bank")
         nc.tensor.transpose(columns_ps[:], rows[:], identity[:])
         columns = held.tile([P, 2 * CB], FP32, name="columns")
         nc.vector.tensor_copy(columns[:], columns_ps[:, 0 : 2 * CB])
 
-        ln_var = held.tile([P, N], FP32, name="ln_var")
-        nc.scalar.activation(ln_var[:], var_ps[:], ACT.Ln, bias=EPS)
-        rstd = held.tile([P, N], FP32, name="rstd")
-        nc.scalar.activation(rstd[:], ln_var[:], ACT.Exp, scale=-0.5)
-
         xn = [held.tile([P, N], BF16, name=f"xn{cb}") for cb in range(CB)]
         for cb in range(CB):
             scaled = held.tile([P, N], FP32, name=f"scaled{cb}")
-            nc.vector.tensor_tensor(scaled[:], centred[cb][:], rstd[:], ALU.mult)
-            nc.scalar.activation(
-                xn[cb][:],
-                scaled[:],
-                ACT.Identity,
-                scale=columns[:, cb : cb + 1],
-                bias=columns[:, CB + cb : CB + cb + 1],
+            nc.vector.scalar_tensor_tensor(
+                scaled[:], centred[cb][:], columns[:, cb : cb + 1], rstd[:], ALU.mult, ALU.mult
             )
+            nc.vector.tensor_scalar_add(xn[cb][:], scaled[:], columns[:, CB + cb : CB + cb + 1])
 
 
         p_ps, q_ps, e_twice, e_squared, turn_part = [], [], [], [], []
@@ -123,67 +141,59 @@ def tile_retnetclm_kernel(tc, base, x, gain, shift, w1, w2, offs, out):
 
         d_minus_1, twice_num_re, twice_num_im_neg = [], [], []
         for fb in range(FB):
-            sine = work.tile([P, N], FP32, name="sine")
-            nc.scalar.activation(sine[:], turn_part[fb][:], ACT.Sin, scale=TWO_PI_BELOW)
-            turn_part_abs = work.tile([P, N], FP32, name="turn_part_abs")
+            turn_part_abs = work.tile([P, N], FP32, name="turn_part_abs", bufs=FB)
             nc.scalar.activation(turn_part_abs[:], turn_part[fb][:], ACT.Abs)
-            cosine = work.tile([P, N], FP32, name="cosine")
+            sine = work.tile([P, N], FP32, name="sine", bufs=FB)
+            nc.scalar.activation(sine[:], turn_part[fb][:], ACT.Sin, scale=TWO_PI_BELOW)
+            cosine = work.tile([P, N], FP32, name="cosine", bufs=FB)
             nc.scalar.activation(
                 cosine[:], turn_part_abs[:], ACT.Sin, scale=-TWO_PI_BELOW, bias=math.pi / 2.0
             )
 
-            x2 = work.tile([P, N], FP32, name="x2")
-            nc.vector.scalar_tensor_tensor(
-                x2[:], e_twice[fb][:], 2.0 * E_CAP, cosine[:], ALU.min, ALU.mult
-            )
             y2 = work.tile([P, N], FP32, name="y2")
             nc.vector.scalar_tensor_tensor(
                 y2[:], e_twice[fb][:], 2.0 * E_CAP, sine[:], ALU.min, ALU.mult
             )
+            x2 = work.tile([P, N], FP32, name="x2")
+            nc.vector.scalar_tensor_tensor(
+                x2[:], e_twice[fb][:], 2.0 * E_CAP, cosine[:], ALU.min, ALU.mult
+            )
+            y2_q = work.tile([P, N], FP32, name="y2_q")
+            nc.vector.tensor_tensor(y2_q[:], y2[:], q_ps[fb][:], ALU.mult)
             d_minus_1.append(work.tile([P, N], FP32, name="d_minus_1", bufs=FB))
             nc.vector.scalar_tensor_tensor(
                 d_minus_1[fb][:], e_squared[fb][:], E_CAP * E_CAP, x2[:], ALU.min, ALU.add
             )
-
             u2_p = work.tile([P, N], FP32, name="u2_p")
             nc.vector.scalar_tensor_tensor(u2_p[:], x2[:], 2.0, p_ps[fb][:], ALU.add, ALU.mult)
-            y2_q = work.tile([P, N], FP32, name="y2_q")
-            nc.vector.tensor_tensor(y2_q[:], y2[:], q_ps[fb][:], ALU.mult)
-            twice_num_re.append(work.tile([P, N], FP32, name="twice_num_re", bufs=FB))
-            nc.vector.tensor_tensor(twice_num_re[fb][:], u2_p[:], y2_q[:], ALU.subtract)
-
-            y2_p = work.tile([P, N], FP32, name="y2_p")
-            nc.vector.tensor_tensor(y2_p[:], y2[:], p_ps[fb][:], ALU.mult)
+            y2_p_neg = work.tile([P, N], FP32, name="y2_p_neg")
+            nc.vector.scalar_tensor_tensor(y2_p_neg[:], y2[:], -1.0, p_ps[fb][:], ALU.mult, ALU.mult)
             u2_q = work.tile([P, N], FP32, name="u2_q")
             nc.vector.scalar_tensor_tensor(u2_q[:], x2[:], 2.0, q_ps[fb][:], ALU.add, ALU.mult)
+            twice_num_re.append(work.tile([P, N], FP32, name="twice_num_re", bufs=FB))
+            nc.gpsimd.tensor_tensor(twice_num_re[fb][:], u2_p[:], y2_q[:], ALU.subtract)
             twice_num_im_neg.append(work.tile([P, N], FP32, name="twice_num_im_neg", bufs=FB))
-            nc.vector.scalar_tensor_tensor(
-                twice_num_im_neg[fb][:], y2_p[:], -1.0, u2_q[:], ALU.mult, ALU.subtract
-            )
-
-        ln_d = []
-        for fb in range(FB):
-            ln_d.append(work.tile([P, N], FP32, name="ln_d", bufs=FB))
-            nc.scalar.activation(ln_d[fb][:], d_minus_1[fb][:], ACT.Ln, bias=1.0)
+            nc.gpsimd.tensor_tensor(twice_num_im_neg[fb][:], y2_p_neg[:], u2_q[:], ALU.subtract)
 
         y_ps = [banks.tile([P, N], FP32, name=f"y_ps{cb}", tag="bank") for cb in range(CB)]
         for fb in range(FB):
+            rsqrt_d = work.tile([P, N], FP32, name="rsqrt_d")
+            nc.scalar.activation(rsqrt_d[:], d_minus_1[fb][:], ACT.Abs_reciprocal_sqrt, bias=1.0)
             half_over_d = work.tile([P, N], FP32, name="half_over_d")
-            nc.scalar.activation(
-                half_over_d[:], ln_d[fb][:], ACT.Exp, scale=-1.0, bias=-math.log(2.0)
-            )
+            nc.scalar.activation(half_over_d[:], rsqrt_d[:], ACT.Square, scale=math.sqrt(0.5))
             a_re = work.tile([P, N], BF16, name="a_re")
             nc.vector.tensor_tensor(a_re[:], twice_num_re[fb][:], half_over_d[:], ALU.mult)
             a_im_neg = work.tile([P, N], BF16, name="a_im_neg")
             nc.vector.tensor_tensor(a_im_neg[:], twice_num_im_neg[fb][:], half_over_d[:], ALU.mult)
-            for cb in range(CB):
-                channels = slice(cb * P, (cb + 1) * P)
-                nc.tensor.matmul(
-                    y_ps[cb][:], w2_sb[:, fb, channels], a_re[:], start=(fb == 0), stop=False
-                )
-                nc.tensor.matmul(
-                    y_ps[cb][:], w2_sb[:, FB + fb, channels], a_im_neg[:], start=False, stop=(fb == FB - 1)
-                )
+            for a_part, w2_block in ((a_re, fb), (a_im_neg, FB + fb)):
+                for cb in range(CB):
+                    nc.tensor.matmul(
+                        y_ps[cb][:],
+                        w2_sb[:, w2_block, cb * P : (cb + 1) * P],
+                        a_part[:],
+                        start=(w2_block == 0),
+                        stop=(w2_block == 2 * FB - 1),
+                    )
 
         for cb in range(CB):
             y_sb = held.tile([P, N], FP32, name=f"y_sb{cb}")
@@ -191,4 +201,5 @@ def tile_retnetclm_kernel(tc, base, x, gain, shift, w1, w2, offs, out):
             nc.vector.tensor_tensor(
                 window[cb][:].indirect(offsets[:]), y_sb[:], x_sb[cb][:], ALU.add
             )
-            nc.sync.dma_start(out[cb * P : (cb + 1) * P, :], window[cb][:])
+            store_queue = (nc.sync, nc.scalar)[cb]
+            store_queue.dma_start(out[cb * P : (cb + 1) * P, :], window[cb][:])

@@ -139,7 +139,7 @@ def tile_retnetclm_kernel(tc, base, x, gain, shift, w1, w2, offs, out):
                 turn_part[fb][:], q_ps[fb][:], TURNS_PER_Q, whole_turns[:], ALU.mult, ALU.subtract
             )
 
-        d_minus_1, twice_num_re, twice_num_im_neg = [], [], []
+        x2, y2, d_minus_1 = [], [], []
         for fb in range(FB):
             turn_part_abs = work.tile([P, N], FP32, name="turn_part_abs", bufs=FB)
             nc.scalar.activation(turn_part_abs[:], turn_part[fb][:], ACT.Abs)
@@ -149,29 +149,34 @@ def tile_retnetclm_kernel(tc, base, x, gain, shift, w1, w2, offs, out):
             nc.scalar.activation(
                 cosine[:], turn_part_abs[:], ACT.Sin, scale=-TWO_PI_BELOW, bias=math.pi / 2.0
             )
-
-            y2 = work.tile([P, N], FP32, name="y2")
+            y2.append(work.tile([P, N], FP32, name="y2", bufs=FB))
             nc.vector.scalar_tensor_tensor(
-                y2[:], e_twice[fb][:], 2.0 * E_CAP, sine[:], ALU.min, ALU.mult
+                y2[fb][:], e_twice[fb][:], 2.0 * E_CAP, sine[:], ALU.min, ALU.mult
             )
-            x2 = work.tile([P, N], FP32, name="x2")
+            x2.append(work.tile([P, N], FP32, name="x2", bufs=FB))
             nc.vector.scalar_tensor_tensor(
-                x2[:], e_twice[fb][:], 2.0 * E_CAP, cosine[:], ALU.min, ALU.mult
+                x2[fb][:], e_twice[fb][:], 2.0 * E_CAP, cosine[:], ALU.min, ALU.mult
             )
-            y2_q = work.tile([P, N], FP32, name="y2_q")
-            nc.vector.tensor_tensor(y2_q[:], y2[:], q_ps[fb][:], ALU.mult)
+        for fb in range(FB):
             d_minus_1.append(work.tile([P, N], FP32, name="d_minus_1", bufs=FB))
             nc.vector.scalar_tensor_tensor(
-                d_minus_1[fb][:], e_squared[fb][:], E_CAP * E_CAP, x2[:], ALU.min, ALU.add
+                d_minus_1[fb][:], e_squared[fb][:], E_CAP * E_CAP, x2[fb][:], ALU.min, ALU.add
             )
+
+        twice_num_re, twice_num_im_neg = [], []
+        for fb in range(FB):
             u2_p = work.tile([P, N], FP32, name="u2_p")
-            nc.vector.scalar_tensor_tensor(u2_p[:], x2[:], 2.0, p_ps[fb][:], ALU.add, ALU.mult)
-            y2_p_neg = work.tile([P, N], FP32, name="y2_p_neg")
-            nc.vector.scalar_tensor_tensor(y2_p_neg[:], y2[:], -1.0, p_ps[fb][:], ALU.mult, ALU.mult)
-            u2_q = work.tile([P, N], FP32, name="u2_q")
-            nc.vector.scalar_tensor_tensor(u2_q[:], x2[:], 2.0, q_ps[fb][:], ALU.add, ALU.mult)
+            nc.vector.scalar_tensor_tensor(u2_p[:], x2[fb][:], 2.0, p_ps[fb][:], ALU.add, ALU.mult)
+            y2_q = work.tile([P, N], FP32, name="y2_q")
+            nc.vector.tensor_tensor(y2_q[:], y2[fb][:], q_ps[fb][:], ALU.mult)
             twice_num_re.append(work.tile([P, N], FP32, name="twice_num_re", bufs=FB))
             nc.gpsimd.tensor_tensor(twice_num_re[fb][:], u2_p[:], y2_q[:], ALU.subtract)
+            y2_p_neg = work.tile([P, N], FP32, name="y2_p_neg")
+            nc.vector.scalar_tensor_tensor(
+                y2_p_neg[:], y2[fb][:], -1.0, p_ps[fb][:], ALU.mult, ALU.mult
+            )
+            u2_q = work.tile([P, N], FP32, name="u2_q")
+            nc.vector.scalar_tensor_tensor(u2_q[:], x2[fb][:], 2.0, q_ps[fb][:], ALU.add, ALU.mult)
             twice_num_im_neg.append(work.tile([P, N], FP32, name="twice_num_im_neg", bufs=FB))
             nc.gpsimd.tensor_tensor(twice_num_im_neg[fb][:], y2_p_neg[:], u2_q[:], ALU.subtract)
 

@@ -165,12 +165,13 @@ def tile_retnetclm_kernel(tc, base, x, gain, shift, w1, w2, offs, out):
 
         twice_num_re, twice_num_im_neg = [], []
         for fb in range(FB):
+            difference_engine = nc.gpsimd if fb < FB - 1 else nc.vector
             u2_p = work.tile([P, N], FP32, name="u2_p")
             nc.vector.scalar_tensor_tensor(u2_p[:], x2[fb][:], 2.0, p_ps[fb][:], ALU.add, ALU.mult)
             y2_q = work.tile([P, N], FP32, name="y2_q")
             nc.vector.tensor_tensor(y2_q[:], y2[fb][:], q_ps[fb][:], ALU.mult)
             twice_num_re.append(work.tile([P, N], FP32, name="twice_num_re", bufs=FB))
-            nc.gpsimd.tensor_tensor(twice_num_re[fb][:], u2_p[:], y2_q[:], ALU.subtract)
+            difference_engine.tensor_tensor(twice_num_re[fb][:], u2_p[:], y2_q[:], ALU.subtract)
             y2_p_neg = work.tile([P, N], FP32, name="y2_p_neg")
             nc.vector.scalar_tensor_tensor(
                 y2_p_neg[:], y2[fb][:], -1.0, p_ps[fb][:], ALU.mult, ALU.mult
@@ -178,7 +179,9 @@ def tile_retnetclm_kernel(tc, base, x, gain, shift, w1, w2, offs, out):
             u2_q = work.tile([P, N], FP32, name="u2_q")
             nc.vector.scalar_tensor_tensor(u2_q[:], x2[fb][:], 2.0, q_ps[fb][:], ALU.add, ALU.mult)
             twice_num_im_neg.append(work.tile([P, N], FP32, name="twice_num_im_neg", bufs=FB))
-            nc.gpsimd.tensor_tensor(twice_num_im_neg[fb][:], y2_p_neg[:], u2_q[:], ALU.subtract)
+            difference_engine.tensor_tensor(
+                twice_num_im_neg[fb][:], y2_p_neg[:], u2_q[:], ALU.subtract
+            )
 
         y_ps = [banks.tile([P, N], FP32, name=f"y_ps{cb}", tag="bank") for cb in range(CB)]
         for fb in range(FB):

@@ -114,7 +114,7 @@ def tile_retnetclm_kernel(tc, base, x, gain, shift, w1, w2, offs, out):
             nc.vector.tensor_scalar_add(xn[cb][:], scaled[:], columns[:, CB + cb : CB + cb + 1])
 
 
-        p_ps, q_ps, e_twice, e_squared, turn_part = [], [], [], [], []
+        p_ps, q_ps, e_twice, e_squared, turn_part, turn_part_abs = [], [], [], [], [], []
         for fb in range(FB):
             p_ps.append(banks.tile([P, N], FP32, name="p_ps", tag="bank"))
             q_ps.append(banks.tile([P, N], FP32, name="q_ps", tag="bank"))
@@ -138,16 +138,18 @@ def tile_retnetclm_kernel(tc, base, x, gain, shift, w1, w2, offs, out):
             nc.vector.scalar_tensor_tensor(
                 turn_part[fb][:], q_ps[fb][:], TURNS_PER_Q, whole_turns[:], ALU.mult, ALU.subtract
             )
+            turn_part_abs.append(work.tile([P, N], FP32, name="turn_part_abs", bufs=FB))
+            nc.vector.scalar_tensor_tensor(
+                turn_part_abs[fb][:], turn_part[fb][:], -1.0, turn_part[fb][:], ALU.mult, ALU.max
+            )
 
         x2, y2, d_minus_1 = [], [], []
         for fb in range(FB):
-            turn_part_abs = work.tile([P, N], FP32, name="turn_part_abs", bufs=FB)
-            nc.scalar.activation(turn_part_abs[:], turn_part[fb][:], ACT.Abs)
             sine = work.tile([P, N], FP32, name="sine", bufs=FB)
             nc.scalar.activation(sine[:], turn_part[fb][:], ACT.Sin, scale=TWO_PI_BELOW)
             cosine = work.tile([P, N], FP32, name="cosine", bufs=FB)
             nc.scalar.activation(
-                cosine[:], turn_part_abs[:], ACT.Sin, scale=-TWO_PI_BELOW, bias=math.pi / 2.0
+                cosine[:], turn_part_abs[fb][:], ACT.Sin, scale=-TWO_PI_BELOW, bias=math.pi / 2.0
             )
             y2.append(work.tile([P, N], FP32, name="y2", bufs=FB))
             nc.vector.scalar_tensor_tensor(

@@ -1,7 +1,6 @@
 import math
 
 import concourse.mybir as mybir
-from concourse.masks import make_identity
 
 FP32 = mybir.dt.float32
 BF16 = mybir.dt.bfloat16
@@ -22,8 +21,6 @@ FLOPS = 2 * C * (2 * F) * N + 2 * (2 * F) * C * N
 TURNS_PER_Q = ALPHA / (2.0 * math.pi)
 TWO_PI_BELOW = 6.2831850051879883
 
-E_CAP = 2.0**31
-
 
 def tile_retnetclm_kernel(tc, base, x, gain, shift, w1, w2, offs, out):
     nc = tc.nc
@@ -39,10 +36,10 @@ def tile_retnetclm_kernel(tc, base, x, gain, shift, w1, w2, offs, out):
         offsets = held.tile([P, N // 16], U16, name="offsets")
         nc.sync.dma_start(offsets[:], offs)
 
-        rows = held.tile([64, P], FP32, name="rows")
-        nc.gpsimd.memset(rows[:], 0.0)
-        nc.sync.dma_start(rows[0:CB, :], gain.rearrange("(b p) o -> b (p o)", p=P))
-        nc.scalar.dma_start(rows[CB : 2 * CB, :], shift.rearrange("(b p) o -> b (p o)", p=P))
+        gain_sb = held.tile([P, CB], FP32, name="gain_sb")
+        nc.sync.dma_start(gain_sb[:], gain.rearrange("(b p) o -> p (b o)", p=P))
+        shift_sb = held.tile([P, CB], FP32, name="shift_sb")
+        nc.scalar.dma_start(shift_sb[:], shift.rearrange("(b p) o -> p (b o)", p=P))
 
         w1_sb = [held.tile([P, 2 * F], BF16, name=f"w1_sb{cb}") for cb in range(CB)]
         nc.sync.dma_start(w1_sb[0][:], w1[0:P, :])
@@ -56,8 +53,6 @@ def tile_retnetclm_kernel(tc, base, x, gain, shift, w1, w2, offs, out):
 
         mean_weights = held.tile([P, P], FP32, name="mean_weights")
         nc.vector.memset(mean_weights[:], 1.0 / C)
-        identity = held.tile([64, 64], FP32, name="identity")
-        make_identity(nc, identity[:])
 
         half_columns = [slice(half * (N // 2), (half + 1) * (N // 2)) for half in range(2)]
         x_sum = held.tile([P, N], FP32, name="x_sum")
@@ -100,25 +95,33 @@ def tile_retnetclm_kernel(tc, base, x, gain, shift, w1, w2, offs, out):
                 rstd[:, columns_of_half], var_ps[:], ACT.Abs_reciprocal_sqrt, bias=EPS
             )
 
-        columns_ps = banks.tile([P, 64], FP32, name="columns_ps", tag="bank")
-        nc.tensor.transpose(columns_ps[:], rows[:], identity[:])
-        columns = held.tile([P, 2 * CB], FP32, name="columns")
-        nc.vector.tensor_copy(columns[:], columns_ps[:, 0 : 2 * CB])
-
         xn = [held.tile([P, N], BF16, name=f"xn{cb}") for cb in range(CB)]
-        for cb in range(CB):
-            scaled = held.tile([P, N], FP32, name=f"scaled{cb}")
-            nc.vector.scalar_tensor_tensor(
-                scaled[:], centred[cb][:], columns[:, cb : cb + 1], rstd[:], ALU.mult, ALU.mult
-            )
-            nc.vector.tensor_scalar_add(xn[cb][:], scaled[:], columns[:, CB + cb : CB + cb + 1])
+        scaled = [held.tile([P, N], FP32, name=f"scaled{cb}") for cb in range(CB)]
+        for columns_of_half in half_columns:
+            for cb in range(CB):
+                nc.vector.scalar_tensor_tensor(
+                    scaled[cb][:, columns_of_half],
+                    centred[cb][:, columns_of_half],
+                    gain_sb[:, cb : cb + 1],
+                    rstd[:, columns_of_half],
+                    ALU.mult,
+                    ALU.mult,
+                )
+            for cb in range(CB):
+                nc.vector.tensor_scalar_add(
+                    xn[cb][:, columns_of_half],
+                    scaled[cb][:, columns_of_half],
+                    shift_sb[:, cb : cb + 1],
+                )
 
+        table_choice = held.tile([P, 1], FP32, name="table_choice")
+        nc.scalar.activation(table_choice[:], rstd[:, N - 1 : N], ACT.Silu)
 
-        p_ps, q_ps, e_twice, e_squared, turn_part, turn_part_abs = [], [], [], [], [], []
+        p_ps, q_ps, turn_part = [], [], []
         for fb in range(FB):
-            p_ps.append(banks.tile([P, N], FP32, name="p_ps", tag="bank"))
             q_ps.append(banks.tile([P, N], FP32, name="q_ps", tag="bank"))
-            for h_ps, first_column in ((p_ps[fb], fb * P), (q_ps[fb], F + fb * P)):
+            p_ps.append(banks.tile([P, N], FP32, name="p_ps", tag="bank"))
+            for h_ps, first_column in ((q_ps[fb], F + fb * P), (p_ps[fb], fb * P)):
                 for cb in range(CB):
                     nc.tensor.matmul(
                         h_ps[:],
@@ -127,63 +130,62 @@ def tile_retnetclm_kernel(tc, base, x, gain, shift, w1, w2, offs, out):
                         start=(cb == 0),
                         stop=(cb == CB - 1),
                     )
-            e_twice.append(work.tile([P, N], FP32, name="e_twice", bufs=FB))
-            nc.scalar.activation(e_twice[fb][:], p_ps[fb][:], ACT.Exp, scale=-ALPHA, bias=math.log(2.0))
-            e_squared.append(work.tile([P, N], FP32, name="e_squared", bufs=FB))
-            nc.scalar.activation(e_squared[fb][:], p_ps[fb][:], ACT.Exp, scale=-2.0 * ALPHA)
+        whole_turns = []
+        for fb in range(FB + 1):
+            if fb < FB:
+                whole_turns.append(work.tile([P, N], I32, name="whole_turns"))
+                nc.vector.tensor_scalar(whole_turns[fb][:], q_ps[fb][:], TURNS_PER_Q, None, ALU.mult)
+            if fb > 0:
+                turn_part.append(work.tile([P, N], FP32, name="turn_part", bufs=FB))
+                nc.vector.scalar_tensor_tensor(
+                    turn_part[fb - 1][:],
+                    q_ps[fb - 1][:],
+                    TURNS_PER_Q,
+                    whole_turns[fb - 1][:],
+                    ALU.mult,
+                    ALU.subtract,
+                )
 
-            whole_turns = work.tile([P, N], I32, name="whole_turns")
-            nc.vector.tensor_scalar(whole_turns[:], q_ps[fb][:], TURNS_PER_Q, None, ALU.mult)
-            turn_part.append(work.tile([P, N], FP32, name="turn_part", bufs=FB))
-            nc.vector.scalar_tensor_tensor(
-                turn_part[fb][:], q_ps[fb][:], TURNS_PER_Q, whole_turns[:], ALU.mult, ALU.subtract
-            )
-            turn_part_abs.append(work.tile([P, N], FP32, name="turn_part_abs", bufs=FB))
-            nc.vector.scalar_tensor_tensor(
-                turn_part_abs[fb][:], turn_part[fb][:], -1.0, turn_part[fb][:], ALU.mult, ALU.max
-            )
-
-        x2, y2, d_minus_1 = [], [], []
+        d_minus_1, n_term, a_term = [], [], []
         for fb in range(FB):
+            tanh_half = work.tile([P, N], FP32, name="tanh_half", bufs=FB)
+            nc.scalar.activation(tanh_half[:], p_ps[fb][:], ACT.Tanh, scale=ALPHA / 2.0)
+            sine_half = work.tile([P, N], FP32, name="sine_half", bufs=FB)
+            nc.scalar.activation(sine_half[:], turn_part[fb][:], ACT.Sin, scale=TWO_PI_BELOW / 2.0)
+            tanh_squared = work.tile([P, N], FP32, name="tanh_squared", bufs=FB)
+            nc.scalar.activation(tanh_squared[:], tanh_half[:], ACT.Square)
+            sine_half_squared = work.tile([P, N], FP32, name="sine_half_squared", bufs=FB)
+            nc.scalar.activation(sine_half_squared[:], sine_half[:], ACT.Square)
             sine = work.tile([P, N], FP32, name="sine", bufs=FB)
             nc.scalar.activation(sine[:], turn_part[fb][:], ACT.Sin, scale=TWO_PI_BELOW)
-            cosine = work.tile([P, N], FP32, name="cosine", bufs=FB)
-            nc.scalar.activation(
-                cosine[:], turn_part_abs[fb][:], ACT.Sin, scale=-TWO_PI_BELOW, bias=math.pi / 2.0
-            )
-            y2.append(work.tile([P, N], FP32, name="y2", bufs=FB))
-            nc.vector.scalar_tensor_tensor(
-                y2[fb][:], e_twice[fb][:], 2.0 * E_CAP, sine[:], ALU.min, ALU.mult
-            )
-            x2.append(work.tile([P, N], FP32, name="x2", bufs=FB))
-            nc.vector.scalar_tensor_tensor(
-                x2[fb][:], e_twice[fb][:], 2.0 * E_CAP, cosine[:], ALU.min, ALU.mult
-            )
-        for fb in range(FB):
             d_minus_1.append(work.tile([P, N], FP32, name="d_minus_1", bufs=FB))
             nc.vector.scalar_tensor_tensor(
-                d_minus_1[fb][:], e_squared[fb][:], E_CAP * E_CAP, x2[fb][:], ALU.min, ALU.add
+                d_minus_1[fb][:], tanh_squared[:], -1.0, sine_half_squared[:], ALU.add, ALU.mult
+            )
+            n_term.append(work.tile([P, N], FP32, name="n_term", bufs=FB))
+            nc.vector.scalar_tensor_tensor(
+                n_term[fb][:], tanh_squared[:], -1.0, sine[:], ALU.add, ALU.mult
+            )
+            a_term.append(work.tile([P, N], FP32, name="a_term", bufs=FB))
+            nc.vector.scalar_tensor_tensor(
+                a_term[fb][:], tanh_half[:], 1.0, d_minus_1[fb][:], ALU.add, ALU.add
             )
 
-        twice_num_re, twice_num_im_neg = [], []
+        num_re, num_im_neg = [], []
         for fb in range(FB):
-            difference_engine = nc.gpsimd if fb < FB - 1 else nc.vector
-            u2_p = work.tile([P, N], FP32, name="u2_p")
-            nc.vector.scalar_tensor_tensor(u2_p[:], x2[fb][:], 2.0, p_ps[fb][:], ALU.add, ALU.mult)
-            y2_q = work.tile([P, N], FP32, name="y2_q")
-            nc.vector.tensor_tensor(y2_q[:], y2[fb][:], q_ps[fb][:], ALU.mult)
-            twice_num_re.append(work.tile([P, N], FP32, name="twice_num_re", bufs=FB))
-            difference_engine.tensor_tensor(twice_num_re[fb][:], u2_p[:], y2_q[:], ALU.subtract)
-            y2_p_neg = work.tile([P, N], FP32, name="y2_p_neg")
-            nc.vector.scalar_tensor_tensor(
-                y2_p_neg[:], y2[fb][:], -1.0, p_ps[fb][:], ALU.mult, ALU.mult
-            )
-            u2_q = work.tile([P, N], FP32, name="u2_q")
-            nc.vector.scalar_tensor_tensor(u2_q[:], x2[fb][:], 2.0, q_ps[fb][:], ALU.add, ALU.mult)
-            twice_num_im_neg.append(work.tile([P, N], FP32, name="twice_num_im_neg", bufs=FB))
-            difference_engine.tensor_tensor(
-                twice_num_im_neg[fb][:], y2_p_neg[:], u2_q[:], ALU.subtract
-            )
+            sum_engine = nc.gpsimd if fb < FB - 1 else nc.vector
+            a_p = work.tile([P, N], FP32, name="a_p")
+            nc.vector.tensor_tensor(a_p[:], a_term[fb][:], p_ps[fb][:], ALU.mult)
+            n_q = work.tile([P, N], FP32, name="n_q")
+            nc.vector.scalar_tensor_tensor(n_q[:], n_term[fb][:], 0.5, q_ps[fb][:], ALU.mult, ALU.mult)
+            num_re.append(work.tile([P, N], FP32, name="num_re", bufs=FB))
+            sum_engine.tensor_tensor(num_re[fb][:], a_p[:], n_q[:], ALU.add)
+            n_p = work.tile([P, N], FP32, name="n_p")
+            nc.vector.scalar_tensor_tensor(n_p[:], n_term[fb][:], 0.5, p_ps[fb][:], ALU.mult, ALU.mult)
+            a_q = work.tile([P, N], FP32, name="a_q")
+            nc.vector.tensor_tensor(a_q[:], a_term[fb][:], q_ps[fb][:], ALU.mult)
+            num_im_neg.append(work.tile([P, N], FP32, name="num_im_neg", bufs=FB))
+            sum_engine.tensor_tensor(num_im_neg[fb][:], n_p[:], a_q[:], ALU.subtract)
 
         y_ps = [banks.tile([P, N], FP32, name=f"y_ps{cb}", tag="bank") for cb in range(CB)]
         for fb in range(FB):
@@ -192,9 +194,9 @@ def tile_retnetclm_kernel(tc, base, x, gain, shift, w1, w2, offs, out):
             half_over_d = work.tile([P, N], FP32, name="half_over_d")
             nc.scalar.activation(half_over_d[:], rsqrt_d[:], ACT.Square, scale=math.sqrt(0.5))
             a_re = work.tile([P, N], BF16, name="a_re")
-            nc.vector.tensor_tensor(a_re[:], twice_num_re[fb][:], half_over_d[:], ALU.mult)
+            nc.vector.tensor_tensor(a_re[:], num_re[fb][:], half_over_d[:], ALU.mult)
             a_im_neg = work.tile([P, N], BF16, name="a_im_neg")
-            nc.vector.tensor_tensor(a_im_neg[:], twice_num_im_neg[fb][:], half_over_d[:], ALU.mult)
+            nc.vector.tensor_tensor(a_im_neg[:], num_im_neg[fb][:], half_over_d[:], ALU.mult)
             for a_part, w2_block in ((a_re, fb), (a_im_neg, FB + fb)):
                 for cb in range(CB):
                     nc.tensor.matmul(

@@ -13,6 +13,7 @@ P = 128
 C, F, S, N = 256, 512, 2048, 512
 CB = C // P
 FB = F // P
+NORM_PIECES = 4
 EPS = 1e-8
 ALPHA = 1.702
 
@@ -26,7 +27,7 @@ def tile_retnetclm_kernel(tc, base, x, gain, shift, w1, w2, offs, out):
     nc = tc.nc
     with (
         tc.tile_pool(name="held", bufs=1) as held,
-        tc.tile_pool(name="work", bufs=2) as work,
+        tc.tile_pool(name="work", bufs=FB) as work,
         tc.psum_pool(name="banks", bufs=8) as banks,
     ):
         x_sb = [held.tile([P, N], FP32, name=f"x_sb{cb}") for cb in range(CB)]
@@ -54,63 +55,66 @@ def tile_retnetclm_kernel(tc, base, x, gain, shift, w1, w2, offs, out):
         mean_weights = held.tile([P, P], FP32, name="mean_weights")
         nc.vector.memset(mean_weights[:], 1.0 / C)
 
-        half_columns = [slice(half * (N // 2), (half + 1) * (N // 2)) for half in range(2)]
+        piece_columns = [
+            slice(piece * (N // NORM_PIECES), (piece + 1) * (N // NORM_PIECES))
+            for piece in range(NORM_PIECES)
+        ]
         x_sum = held.tile([P, N], FP32, name="x_sum")
         mean_ps = []
-        for columns_of_half in half_columns:
+        for columns_of_piece in piece_columns:
             nc.vector.tensor_tensor(
-                x_sum[:, columns_of_half], x_sb[0][:, columns_of_half], x_sb[1][:, columns_of_half], ALU.add
+                x_sum[:, columns_of_piece], x_sb[0][:, columns_of_piece], x_sb[1][:, columns_of_piece], ALU.add
             )
-            mean_ps.append(banks.tile([P, N // 2], FP32, name="mean_ps", tag="bank"))
+            mean_ps.append(banks.tile([P, N // NORM_PIECES], FP32, name="mean_ps", tag="bank"))
             nc.tensor.matmul(
-                mean_ps[-1][:], mean_weights[:], x_sum[:, columns_of_half], start=True, stop=True
+                mean_ps[-1][:], mean_weights[:], x_sum[:, columns_of_piece], start=True, stop=True
             )
         centred = [held.tile([P, N], FP32, name=f"centred{cb}") for cb in range(CB)]
         squared = [held.tile([P, N], FP32, name=f"squared{cb}") for cb in range(CB)]
         squared_sum = held.tile([P, N], FP32, name="squared_sum")
         rstd = held.tile([P, N], FP32, name="rstd")
-        for half, columns_of_half in enumerate(half_columns):
+        for piece, columns_of_piece in enumerate(piece_columns):
             for cb in range(CB):
                 nc.vector.tensor_tensor(
-                    centred[cb][:, columns_of_half], x_sb[cb][:, columns_of_half], mean_ps[half][:], ALU.subtract
+                    centred[cb][:, columns_of_piece], x_sb[cb][:, columns_of_piece], mean_ps[piece][:], ALU.subtract
                 )
             for cb in range(CB):
                 nc.vector.tensor_tensor(
-                    squared[cb][:, columns_of_half],
-                    centred[cb][:, columns_of_half],
-                    centred[cb][:, columns_of_half],
+                    squared[cb][:, columns_of_piece],
+                    centred[cb][:, columns_of_piece],
+                    centred[cb][:, columns_of_piece],
                     ALU.mult,
                 )
             nc.vector.tensor_tensor(
-                squared_sum[:, columns_of_half],
-                squared[0][:, columns_of_half],
-                squared[1][:, columns_of_half],
+                squared_sum[:, columns_of_piece],
+                squared[0][:, columns_of_piece],
+                squared[1][:, columns_of_piece],
                 ALU.add,
             )
-            var_ps = banks.tile([P, N // 2], FP32, name="var_ps", tag="bank")
+            var_ps = banks.tile([P, N // NORM_PIECES], FP32, name="var_ps", tag="bank")
             nc.tensor.matmul(
-                var_ps[:], mean_weights[:], squared_sum[:, columns_of_half], start=True, stop=True
+                var_ps[:], mean_weights[:], squared_sum[:, columns_of_piece], start=True, stop=True
             )
             nc.scalar.activation(
-                rstd[:, columns_of_half], var_ps[:], ACT.Abs_reciprocal_sqrt, bias=EPS
+                rstd[:, columns_of_piece], var_ps[:], ACT.Abs_reciprocal_sqrt, bias=EPS
             )
 
         xn = [held.tile([P, N], BF16, name=f"xn{cb}") for cb in range(CB)]
         scaled = [held.tile([P, N], FP32, name=f"scaled{cb}") for cb in range(CB)]
-        for columns_of_half in half_columns:
+        for columns_of_piece in piece_columns:
             for cb in range(CB):
                 nc.vector.scalar_tensor_tensor(
-                    scaled[cb][:, columns_of_half],
-                    centred[cb][:, columns_of_half],
+                    scaled[cb][:, columns_of_piece],
+                    centred[cb][:, columns_of_piece],
                     gain_sb[:, cb : cb + 1],
-                    rstd[:, columns_of_half],
+                    rstd[:, columns_of_piece],
                     ALU.mult,
                     ALU.mult,
                 )
             for cb in range(CB):
                 nc.vector.tensor_scalar_add(
-                    xn[cb][:, columns_of_half],
-                    scaled[cb][:, columns_of_half],
+                    xn[cb][:, columns_of_piece],
+                    scaled[cb][:, columns_of_piece],
                     shift_sb[:, cb : cb + 1],
                 )
 
@@ -130,45 +134,42 @@ def tile_retnetclm_kernel(tc, base, x, gain, shift, w1, w2, offs, out):
                         start=(cb == 0),
                         stop=(cb == CB - 1),
                     )
-        whole_turns = []
-        for fb in range(FB + 1):
-            if fb < FB:
-                whole_turns.append(work.tile([P, N], I32, name="whole_turns"))
-                nc.vector.tensor_scalar(whole_turns[fb][:], q_ps[fb][:], TURNS_PER_Q, None, ALU.mult)
-            if fb > 0:
-                turn_part.append(work.tile([P, N], FP32, name="turn_part", bufs=FB))
-                nc.vector.scalar_tensor_tensor(
-                    turn_part[fb - 1][:],
-                    q_ps[fb - 1][:],
-                    TURNS_PER_Q,
-                    whole_turns[fb - 1][:],
-                    ALU.mult,
-                    ALU.subtract,
-                )
+        for fb in range(FB):
+            whole_turns = work.tile([P, N], I32, name="whole_turns")
+            nc.vector.tensor_scalar(whole_turns[:], q_ps[fb][:], TURNS_PER_Q, None, ALU.mult)
+            turn_part.append(work.tile([P, N], FP32, name="turn_part"))
+            nc.vector.scalar_tensor_tensor(
+                turn_part[fb][:], q_ps[fb][:], TURNS_PER_Q, whole_turns[:], ALU.mult, ALU.subtract
+            )
 
+        tanh_half, tanh_squared = [], []
+        for fb in range(FB):
+            tanh_half.append(work.tile([P, N], FP32, name="tanh_half"))
+            nc.scalar.activation(tanh_half[fb][:], p_ps[fb][:], ACT.Tanh, scale=ALPHA / 2.0)
+            tanh_squared.append(work.tile([P, N], FP32, name="tanh_squared"))
+            if fb < FB - 1:
+                nc.gpsimd.tensor_tensor(tanh_squared[fb][:], tanh_half[fb][:], tanh_half[fb][:], ALU.mult)
+            else:
+                nc.scalar.activation(tanh_squared[fb][:], tanh_half[fb][:], ACT.Square)
         d_minus_1, n_term, a_term = [], [], []
         for fb in range(FB):
-            tanh_half = work.tile([P, N], FP32, name="tanh_half", bufs=FB)
-            nc.scalar.activation(tanh_half[:], p_ps[fb][:], ACT.Tanh, scale=ALPHA / 2.0)
-            sine_half = work.tile([P, N], FP32, name="sine_half", bufs=FB)
+            sine_half = work.tile([P, N], FP32, name="sine_half")
             nc.scalar.activation(sine_half[:], turn_part[fb][:], ACT.Sin, scale=TWO_PI_BELOW / 2.0)
-            tanh_squared = work.tile([P, N], FP32, name="tanh_squared", bufs=FB)
-            nc.scalar.activation(tanh_squared[:], tanh_half[:], ACT.Square)
-            sine_half_squared = work.tile([P, N], FP32, name="sine_half_squared", bufs=FB)
-            nc.scalar.activation(sine_half_squared[:], sine_half[:], ACT.Square)
-            sine = work.tile([P, N], FP32, name="sine", bufs=FB)
+            sine = work.tile([P, N], FP32, name="sine")
             nc.scalar.activation(sine[:], turn_part[fb][:], ACT.Sin, scale=TWO_PI_BELOW)
-            d_minus_1.append(work.tile([P, N], FP32, name="d_minus_1", bufs=FB))
+            sine_half_squared = work.tile([P, N], FP32, name="sine_half_squared")
+            nc.scalar.activation(sine_half_squared[:], sine_half[:], ACT.Square)
+            d_minus_1.append(work.tile([P, N], FP32, name="d_minus_1"))
             nc.vector.scalar_tensor_tensor(
-                d_minus_1[fb][:], tanh_squared[:], -1.0, sine_half_squared[:], ALU.add, ALU.mult
+                d_minus_1[fb][:], tanh_squared[fb][:], -1.0, sine_half_squared[:], ALU.add, ALU.mult
             )
-            n_term.append(work.tile([P, N], FP32, name="n_term", bufs=FB))
+            n_term.append(work.tile([P, N], FP32, name="n_term"))
             nc.vector.scalar_tensor_tensor(
-                n_term[fb][:], tanh_squared[:], -1.0, sine[:], ALU.add, ALU.mult
+                n_term[fb][:], tanh_squared[fb][:], -1.0, sine[:], ALU.add, ALU.mult
             )
-            a_term.append(work.tile([P, N], FP32, name="a_term", bufs=FB))
+            a_term.append(work.tile([P, N], FP32, name="a_term"))
             nc.vector.scalar_tensor_tensor(
-                a_term[fb][:], tanh_half[:], 1.0, d_minus_1[fb][:], ALU.add, ALU.add
+                a_term[fb][:], tanh_half[fb][:], 1.0, d_minus_1[fb][:], ALU.add, ALU.add
             )
 
         num_re, num_im_neg = [], []
@@ -178,13 +179,13 @@ def tile_retnetclm_kernel(tc, base, x, gain, shift, w1, w2, offs, out):
             nc.vector.tensor_tensor(a_p[:], a_term[fb][:], p_ps[fb][:], ALU.mult)
             n_q = work.tile([P, N], FP32, name="n_q")
             nc.vector.scalar_tensor_tensor(n_q[:], n_term[fb][:], 0.5, q_ps[fb][:], ALU.mult, ALU.mult)
-            num_re.append(work.tile([P, N], FP32, name="num_re", bufs=FB))
+            num_re.append(work.tile([P, N], FP32, name="num_re"))
             sum_engine.tensor_tensor(num_re[fb][:], a_p[:], n_q[:], ALU.add)
             n_p = work.tile([P, N], FP32, name="n_p")
             nc.vector.scalar_tensor_tensor(n_p[:], n_term[fb][:], 0.5, p_ps[fb][:], ALU.mult, ALU.mult)
             a_q = work.tile([P, N], FP32, name="a_q")
             nc.vector.tensor_tensor(a_q[:], a_term[fb][:], q_ps[fb][:], ALU.mult)
-            num_im_neg.append(work.tile([P, N], FP32, name="num_im_neg", bufs=FB))
+            num_im_neg.append(work.tile([P, N], FP32, name="num_im_neg"))
             sum_engine.tensor_tensor(num_im_neg[fb][:], n_p[:], a_q[:], ALU.subtract)
 
         y_ps = [banks.tile([P, N], FP32, name=f"y_ps{cb}", tag="bank") for cb in range(CB)]

@@ -1,6 +1,7 @@
 import math
 
 import concourse.mybir as mybir
+from concourse.masks import make_identity
 
 FP32 = mybir.dt.float32
 BF16 = mybir.dt.bfloat16
@@ -30,9 +31,18 @@ def tile_retnetclm_kernel(tc, base, x, gain, shift, w1, w2, offs, out):
         tc.tile_pool(name="work", bufs=FB) as work,
         tc.psum_pool(name="banks", bufs=8) as banks,
     ):
+        piece_columns = [
+            slice(piece * (N // NORM_PIECES), (piece + 1) * (N // NORM_PIECES))
+            for piece in range(NORM_PIECES)
+        ]
         x_sb = [held.tile([P, N], FP32, name=f"x_sb{cb}") for cb in range(CB)]
-        nc.sync.dma_start(x_sb[0][:], x[0:P, :])
-        nc.scalar.dma_start(x_sb[1][:], x[P : 2 * P, :])
+        for columns_of_piece in piece_columns:
+            nc.sync.dma_start(x_sb[0][:, columns_of_piece], x[0:P, columns_of_piece])
+            nc.scalar.dma_start(x_sb[1][:, columns_of_piece], x[P : 2 * P, columns_of_piece])
+
+        w1_sb = [held.tile([P, 2 * F], BF16, name=f"w1_sb{cb}") for cb in range(CB)]
+        nc.sync.dma_start(w1_sb[0][:], w1[0:P, :])
+        nc.scalar.dma_start(w1_sb[1][:], w1[P : 2 * P, :])
 
         offsets = held.tile([P, N // 16], U16, name="offsets")
         nc.sync.dma_start(offsets[:], offs)
@@ -42,9 +52,6 @@ def tile_retnetclm_kernel(tc, base, x, gain, shift, w1, w2, offs, out):
         shift_sb = held.tile([P, CB], FP32, name="shift_sb")
         nc.scalar.dma_start(shift_sb[:], shift.rearrange("(b p) o -> p (b o)", p=P))
 
-        w1_sb = [held.tile([P, 2 * F], BF16, name=f"w1_sb{cb}") for cb in range(CB)]
-        nc.sync.dma_start(w1_sb[0][:], w1[0:P, :])
-        nc.scalar.dma_start(w1_sb[1][:], w1[P : 2 * P, :])
         w2_sb = held.tile([P, 2 * FB, C], BF16, name="w2_sb")
         nc.sync.dma_start(w2_sb[:], w2.rearrange("(k p) c -> p k c", p=P))
 
@@ -54,11 +61,9 @@ def tile_retnetclm_kernel(tc, base, x, gain, shift, w1, w2, offs, out):
 
         mean_weights = held.tile([P, P], FP32, name="mean_weights")
         nc.vector.memset(mean_weights[:], 1.0 / C)
+        identity = held.tile([P, P], FP32, name="identity")
+        make_identity(nc, identity[:])
 
-        piece_columns = [
-            slice(piece * (N // NORM_PIECES), (piece + 1) * (N // NORM_PIECES))
-            for piece in range(NORM_PIECES)
-        ]
         x_sum = held.tile([P, N], FP32, name="x_sum")
         mean_ps = []
         for columns_of_piece in piece_columns:
@@ -174,30 +179,33 @@ def tile_retnetclm_kernel(tc, base, x, gain, shift, w1, w2, offs, out):
 
         num_re, num_im_neg = [], []
         for fb in range(FB):
-            sum_engine = nc.gpsimd if fb < FB - 1 else nc.vector
             a_p = work.tile([P, N], FP32, name="a_p")
             nc.vector.tensor_tensor(a_p[:], a_term[fb][:], p_ps[fb][:], ALU.mult)
             n_q = work.tile([P, N], FP32, name="n_q")
             nc.vector.scalar_tensor_tensor(n_q[:], n_term[fb][:], 0.5, q_ps[fb][:], ALU.mult, ALU.mult)
             num_re.append(work.tile([P, N], FP32, name="num_re"))
-            sum_engine.tensor_tensor(num_re[fb][:], a_p[:], n_q[:], ALU.add)
+            nc.gpsimd.tensor_tensor(num_re[fb][:], a_p[:], n_q[:], ALU.add)
             n_p = work.tile([P, N], FP32, name="n_p")
             nc.vector.scalar_tensor_tensor(n_p[:], n_term[fb][:], 0.5, p_ps[fb][:], ALU.mult, ALU.mult)
             a_q = work.tile([P, N], FP32, name="a_q")
             nc.vector.tensor_tensor(a_q[:], a_term[fb][:], q_ps[fb][:], ALU.mult)
             num_im_neg.append(work.tile([P, N], FP32, name="num_im_neg"))
-            sum_engine.tensor_tensor(num_im_neg[fb][:], n_p[:], a_q[:], ALU.subtract)
+            nc.gpsimd.tensor_tensor(num_im_neg[fb][:], n_p[:], a_q[:], ALU.subtract)
 
         y_ps = [banks.tile([P, N], FP32, name=f"y_ps{cb}", tag="bank") for cb in range(CB)]
+        half_over_d_ps = []
         for fb in range(FB):
             rsqrt_d = work.tile([P, N], FP32, name="rsqrt_d")
             nc.scalar.activation(rsqrt_d[:], d_minus_1[fb][:], ACT.Abs_reciprocal_sqrt, bias=1.0)
             half_over_d = work.tile([P, N], FP32, name="half_over_d")
             nc.scalar.activation(half_over_d[:], rsqrt_d[:], ACT.Square, scale=math.sqrt(0.5))
+            half_over_d_ps.append(banks.tile([P, N], FP32, name="half_over_d_ps", tag="bank"))
+            nc.tensor.matmul(half_over_d_ps[fb][:], identity[:], half_over_d[:], start=True, stop=True)
+        for fb in range(FB):
             a_re = work.tile([P, N], BF16, name="a_re")
-            nc.vector.tensor_tensor(a_re[:], num_re[fb][:], half_over_d[:], ALU.mult)
+            nc.vector.tensor_tensor(a_re[:], num_re[fb][:], half_over_d_ps[fb][:], ALU.mult)
             a_im_neg = work.tile([P, N], BF16, name="a_im_neg")
-            nc.vector.tensor_tensor(a_im_neg[:], num_im_neg[fb][:], half_over_d[:], ALU.mult)
+            nc.vector.tensor_tensor(a_im_neg[:], num_im_neg[fb][:], half_over_d_ps[fb][:], ALU.mult)
             for a_part, w2_block in ((a_re, fb), (a_im_neg, FB + fb)):
                 for cb in range(CB):
                     nc.tensor.matmul(

@@ -14,7 +14,7 @@ P = 128
 C, F, S, N = 256, 512, 2048, 512
 CB = C // P
 FB = F // P
-NORM_PIECES = 4
+NORM_PIECES = 2
 EPS = 1e-8
 ALPHA = 1.702
 
@@ -216,11 +216,12 @@ def tile_retnetclm_kernel(tc, base, x, gain, shift, w1, w2, offs, out):
                         stop=(w2_block == 2 * FB - 1),
                     )
 
+        copy_of_block = (nc.vector.tensor_copy, nc.scalar.copy)
+        store_queue = (nc.sync, nc.scalar)
         for cb in range(CB):
             y_sb = held.tile([P, N], FP32, name=f"y_sb{cb}")
-            nc.scalar.copy(y_sb[:], y_ps[cb][:])
+            copy_of_block[cb](y_sb[:], y_ps[cb][:])
             nc.vector.tensor_tensor(
                 window[cb][:].indirect(offsets[:]), y_sb[:], x_sb[cb][:], ALU.add
             )
-            store_queue = (nc.sync, nc.scalar)[cb]
-            store_queue.dma_start(out[cb * P : (cb + 1) * P, :], window[cb][:])
+            store_queue[cb].dma_start(out[cb * P : (cb + 1) * P, :], window[cb][:])

@@ -29,7 +29,7 @@ def tile_retnetclm_kernel(tc, base, x, gain, shift, w1, w2, offs, out):
     with (
         tc.tile_pool(name="held", bufs=1) as held,
         tc.tile_pool(name="work", bufs=FB) as work,
-        tc.psum_pool(name="banks", bufs=8) as banks,
+        tc.psum_pool(name="banks", bufs=4) as banks,
     ):
         piece_columns = [
             slice(piece * (N // NORM_PIECES), (piece + 1) * (N // NORM_PIECES))
@@ -70,7 +70,7 @@ def tile_retnetclm_kernel(tc, base, x, gain, shift, w1, w2, offs, out):
             nc.vector.tensor_tensor(
                 x_sum[:, columns_of_piece], x_sb[0][:, columns_of_piece], x_sb[1][:, columns_of_piece], ALU.add
             )
-            mean_ps.append(banks.tile([P, N // NORM_PIECES], FP32, name="mean_ps", tag="bank"))
+            mean_ps.append(banks.tile([P, N // NORM_PIECES], FP32, name="mean_ps", tag="q_side"))
             nc.tensor.matmul(
                 mean_ps[-1][:], mean_weights[:], x_sum[:, columns_of_piece], start=True, stop=True
             )
@@ -96,7 +96,7 @@ def tile_retnetclm_kernel(tc, base, x, gain, shift, w1, w2, offs, out):
                 squared[1][:, columns_of_piece],
                 ALU.add,
             )
-            var_ps = banks.tile([P, N // NORM_PIECES], FP32, name="var_ps", tag="bank")
+            var_ps = banks.tile([P, N // NORM_PIECES], FP32, name="var_ps", tag="p_side")
             nc.tensor.matmul(
                 var_ps[:], mean_weights[:], squared_sum[:, columns_of_piece], start=True, stop=True
             )
@@ -126,37 +126,42 @@ def tile_retnetclm_kernel(tc, base, x, gain, shift, w1, w2, offs, out):
         table_choice = held.tile([P, 1], FP32, name="table_choice")
         nc.scalar.activation(table_choice[:], rstd[:, N - 1 : N], ACT.Silu)
 
-        p_ps, q_ps, turn_part = [], [], []
+
+        def first_layer(h_ps, first_column):
+            for cb in range(CB):
+                nc.tensor.matmul(
+                    h_ps[:],
+                    w1_sb[cb][:, first_column : first_column + P],
+                    xn[cb][:],
+                    start=(cb == 0),
+                    stop=(cb == CB - 1),
+                )
+
+        p_ps, turn_part = [], []
         for fb in range(FB):
-            q_ps.append(banks.tile([P, N], FP32, name="q_ps", tag="bank"))
-            p_ps.append(banks.tile([P, N], FP32, name="p_ps", tag="bank"))
-            for h_ps, first_column in ((q_ps[fb], F + fb * P), (p_ps[fb], fb * P)):
-                for cb in range(CB):
-                    nc.tensor.matmul(
-                        h_ps[:],
-                        w1_sb[cb][:, first_column : first_column + P],
-                        xn[cb][:],
-                        start=(cb == 0),
-                        stop=(cb == CB - 1),
-                    )
-        for fb in range(FB):
+            q_ps = banks.tile([P, N], FP32, name="q_ps", tag="q_side")
+            first_layer(q_ps, F + fb * P)
+            p_ps.append(banks.tile([P, N], FP32, name="p_ps", tag="p_side"))
+            first_layer(p_ps[fb], fb * P)
             whole_turns = work.tile([P, N], I32, name="whole_turns")
-            nc.vector.tensor_scalar(whole_turns[:], q_ps[fb][:], TURNS_PER_Q, None, ALU.mult)
+            nc.vector.tensor_scalar(whole_turns[:], q_ps[:], TURNS_PER_Q, None, ALU.mult)
             turn_part.append(work.tile([P, N], FP32, name="turn_part"))
             nc.vector.scalar_tensor_tensor(
-                turn_part[fb][:], q_ps[fb][:], TURNS_PER_Q, whole_turns[:], ALU.mult, ALU.subtract
+                turn_part[fb][:], q_ps[:], TURNS_PER_Q, whole_turns[:], ALU.mult, ALU.subtract
             )
 
-        tanh_half, tanh_squared = [], []
+        tanh_half, tanh_squared_ps = [], []
         for fb in range(FB):
             tanh_half.append(work.tile([P, N], FP32, name="tanh_half"))
             nc.scalar.activation(tanh_half[fb][:], p_ps[fb][:], ACT.Tanh, scale=ALPHA / 2.0)
-            tanh_squared.append(work.tile([P, N], FP32, name="tanh_squared"))
+            tanh_squared = work.tile([P, N], FP32, name="tanh_squared")
             if fb < FB - 1:
-                nc.gpsimd.tensor_tensor(tanh_squared[fb][:], tanh_half[fb][:], tanh_half[fb][:], ALU.mult)
+                nc.gpsimd.tensor_tensor(tanh_squared[:], tanh_half[fb][:], tanh_half[fb][:], ALU.mult)
             else:
-                nc.scalar.activation(tanh_squared[fb][:], tanh_half[fb][:], ACT.Square)
-        d_minus_1, n_term, a_term = [], [], []
+                nc.scalar.activation(tanh_squared[:], tanh_half[fb][:], ACT.Square)
+            tanh_squared_ps.append(banks.tile([P, N], FP32, name="tanh_squared_ps", tag="q_side"))
+            nc.tensor.matmul(tanh_squared_ps[fb][:], identity[:], tanh_squared[:], start=True, stop=True)
+        d_minus_1, n_term, a_minus_1 = [], [], []
         for fb in range(FB):
             sine_half = work.tile([P, N], FP32, name="sine_half")
             nc.scalar.activation(sine_half[:], turn_part[fb][:], ACT.Sin, scale=TWO_PI_BELOW / 2.0)
@@ -166,41 +171,41 @@ def tile_retnetclm_kernel(tc, base, x, gain, shift, w1, w2, offs, out):
             nc.scalar.activation(sine_half_squared[:], sine_half[:], ACT.Square)
             d_minus_1.append(work.tile([P, N], FP32, name="d_minus_1"))
             nc.vector.scalar_tensor_tensor(
-                d_minus_1[fb][:], tanh_squared[fb][:], -1.0, sine_half_squared[:], ALU.add, ALU.mult
+                d_minus_1[fb][:], tanh_squared_ps[fb][:], -1.0, sine_half_squared[:], ALU.add, ALU.mult
             )
             n_term.append(work.tile([P, N], FP32, name="n_term"))
             nc.vector.scalar_tensor_tensor(
-                n_term[fb][:], tanh_squared[fb][:], -1.0, sine[:], ALU.add, ALU.mult
+                n_term[fb][:], tanh_squared_ps[fb][:], -1.0, sine[:], ALU.add, ALU.mult
             )
-            a_term.append(work.tile([P, N], FP32, name="a_term"))
-            nc.vector.scalar_tensor_tensor(
-                a_term[fb][:], tanh_half[fb][:], 1.0, d_minus_1[fb][:], ALU.add, ALU.add
-            )
+            a_minus_1.append(work.tile([P, N], FP32, name="a_minus_1"))
+            nc.gpsimd.tensor_tensor(a_minus_1[fb][:], tanh_half[fb][:], d_minus_1[fb][:], ALU.add)
 
         num_re, num_im_neg = [], []
         for fb in range(FB):
+            q_ps = banks.tile([P, N], FP32, name="q_ps", tag="q_side")
+            first_layer(q_ps, F + fb * P)
             a_p = work.tile([P, N], FP32, name="a_p")
-            nc.vector.tensor_tensor(a_p[:], a_term[fb][:], p_ps[fb][:], ALU.mult)
+            nc.vector.scalar_tensor_tensor(a_p[:], a_minus_1[fb][:], 1.0, p_ps[fb][:], ALU.add, ALU.mult)
             n_q = work.tile([P, N], FP32, name="n_q")
-            nc.vector.scalar_tensor_tensor(n_q[:], n_term[fb][:], 0.5, q_ps[fb][:], ALU.mult, ALU.mult)
+            nc.vector.scalar_tensor_tensor(n_q[:], n_term[fb][:], 0.5, q_ps[:], ALU.mult, ALU.mult)
             num_re.append(work.tile([P, N], FP32, name="num_re"))
             nc.gpsimd.tensor_tensor(num_re[fb][:], a_p[:], n_q[:], ALU.add)
             n_p = work.tile([P, N], FP32, name="n_p")
             nc.vector.scalar_tensor_tensor(n_p[:], n_term[fb][:], 0.5, p_ps[fb][:], ALU.mult, ALU.mult)
             a_q = work.tile([P, N], FP32, name="a_q")
-            nc.vector.tensor_tensor(a_q[:], a_term[fb][:], q_ps[fb][:], ALU.mult)
+            nc.vector.scalar_tensor_tensor(a_q[:], a_minus_1[fb][:], 1.0, q_ps[:], ALU.add, ALU.mult)
             num_im_neg.append(work.tile([P, N], FP32, name="num_im_neg"))
             nc.gpsimd.tensor_tensor(num_im_neg[fb][:], n_p[:], a_q[:], ALU.subtract)
 
-        y_ps = [banks.tile([P, N], FP32, name=f"y_ps{cb}", tag="bank") for cb in range(CB)]
         half_over_d_ps = []
         for fb in range(FB):
             rsqrt_d = work.tile([P, N], FP32, name="rsqrt_d")
             nc.scalar.activation(rsqrt_d[:], d_minus_1[fb][:], ACT.Abs_reciprocal_sqrt, bias=1.0)
             half_over_d = work.tile([P, N], FP32, name="half_over_d")
             nc.scalar.activation(half_over_d[:], rsqrt_d[:], ACT.Square, scale=math.sqrt(0.5))
-            half_over_d_ps.append(banks.tile([P, N], FP32, name="half_over_d_ps", tag="bank"))
+            half_over_d_ps.append(banks.tile([P, N], FP32, name="half_over_d_ps", tag="q_side"))
             nc.tensor.matmul(half_over_d_ps[fb][:], identity[:], half_over_d[:], start=True, stop=True)
+        y_ps = [banks.tile([P, N], FP32, name=f"y_ps{cb}", tag="p_side") for cb in range(CB)]
         for fb in range(FB):
             a_re = work.tile([P, N], BF16, name="a_re")
             nc.vector.tensor_tensor(a_re[:], num_re[fb][:], half_over_d_ps[fb][:], ALU.mult)

@@ -127,12 +127,12 @@ def tile_retnetclm_kernel(tc, base, x, gain, shift, w1, w2, offs, out):
         nc.scalar.activation(table_choice[:], rstd[:, N - 1 : N], ACT.Silu)
 
 
-        def first_layer(h_ps, first_column):
+        def first_layer(h_ps, first_column, token_columns):
             for cb in range(CB):
                 nc.tensor.matmul(
-                    h_ps[:],
+                    h_ps[:, token_columns],
                     w1_sb[cb][:, first_column : first_column + P],
-                    xn[cb][:],
+                    xn[cb][:, token_columns],
                     start=(cb == 0),
                     stop=(cb == CB - 1),
                 )
@@ -140,9 +140,11 @@ def tile_retnetclm_kernel(tc, base, x, gain, shift, w1, w2, offs, out):
         p_ps, turn_part = [], []
         for fb in range(FB):
             q_ps = banks.tile([P, N], FP32, name="q_ps", tag="q_side")
-            first_layer(q_ps, F + fb * P)
+            for columns_of_piece in piece_columns:
+                first_layer(q_ps, F + fb * P, columns_of_piece)
             p_ps.append(banks.tile([P, N], FP32, name="p_ps", tag="p_side"))
-            first_layer(p_ps[fb], fb * P)
+            for columns_of_piece in piece_columns:
+                first_layer(p_ps[fb], fb * P, columns_of_piece)
             whole_turns = work.tile([P, N], I32, name="whole_turns")
             nc.vector.tensor_scalar(whole_turns[:], q_ps[:], TURNS_PER_Q, None, ALU.mult)
             turn_part.append(work.tile([P, N], FP32, name="turn_part"))
@@ -183,15 +185,15 @@ def tile_retnetclm_kernel(tc, base, x, gain, shift, w1, w2, offs, out):
         num_re, num_im_neg = [], []
         for fb in range(FB):
             q_ps = banks.tile([P, N], FP32, name="q_ps", tag="q_side")
-            first_layer(q_ps, F + fb * P)
+            first_layer(q_ps, F + fb * P, slice(0, N))
+            n_p = work.tile([P, N], FP32, name="n_p")
+            nc.vector.scalar_tensor_tensor(n_p[:], n_term[fb][:], 0.5, p_ps[fb][:], ALU.mult, ALU.mult)
             a_p = work.tile([P, N], FP32, name="a_p")
             nc.vector.scalar_tensor_tensor(a_p[:], a_minus_1[fb][:], 1.0, p_ps[fb][:], ALU.add, ALU.mult)
             n_q = work.tile([P, N], FP32, name="n_q")
             nc.vector.scalar_tensor_tensor(n_q[:], n_term[fb][:], 0.5, q_ps[:], ALU.mult, ALU.mult)
             num_re.append(work.tile([P, N], FP32, name="num_re"))
             nc.gpsimd.tensor_tensor(num_re[fb][:], a_p[:], n_q[:], ALU.add)
-            n_p = work.tile([P, N], FP32, name="n_p")
-            nc.vector.scalar_tensor_tensor(n_p[:], n_term[fb][:], 0.5, p_ps[fb][:], ALU.mult, ALU.mult)
             a_q = work.tile([P, N], FP32, name="a_q")
             nc.vector.scalar_tensor_tensor(a_q[:], a_minus_1[fb][:], 1.0, q_ps[:], ALU.add, ALU.mult)
             num_im_neg.append(work.tile([P, N], FP32, name="num_im_neg"))

@@ -63,6 +63,8 @@ def tile_retnetclm_kernel(tc, base, x, gain, shift, w1, w2, offs, out):
         nc.vector.memset(mean_weights[:], 1.0 / C)
         identity = held.tile([P, P], FP32, name="identity")
         make_identity(nc, identity[:])
+        table_choice = held.tile([P, 1], FP32, name="table_choice")
+        nc.scalar.activation(table_choice[:], mean_weights[:, 0:1], ACT.Abs_reciprocal_sqrt)
 
         x_sum = held.tile([P, N], FP32, name="x_sum")
         mean_ps = []
@@ -76,40 +78,34 @@ def tile_retnetclm_kernel(tc, base, x, gain, shift, w1, w2, offs, out):
             )
         centred = [held.tile([P, N], FP32, name=f"centred{cb}") for cb in range(CB)]
         squared = [held.tile([P, N], FP32, name=f"squared{cb}") for cb in range(CB)]
-        squared_sum = held.tile([P, N], FP32, name="squared_sum")
         rstd = held.tile([P, N], FP32, name="rstd")
         for piece, columns_of_piece in enumerate(piece_columns):
-            for cb in range(CB):
+            for cb in (1, 0):
                 nc.vector.tensor_tensor(
                     centred[cb][:, columns_of_piece], x_sb[cb][:, columns_of_piece], mean_ps[piece][:], ALU.subtract
                 )
-            for cb in range(CB):
-                nc.vector.tensor_tensor(
-                    squared[cb][:, columns_of_piece],
-                    centred[cb][:, columns_of_piece],
-                    centred[cb][:, columns_of_piece],
-                    ALU.mult,
-                )
+            nc.scalar.activation(squared[1][:, columns_of_piece], centred[1][:, columns_of_piece], ACT.Square)
             nc.vector.tensor_tensor(
-                squared_sum[:, columns_of_piece],
                 squared[0][:, columns_of_piece],
-                squared[1][:, columns_of_piece],
-                ALU.add,
+                centred[0][:, columns_of_piece],
+                centred[0][:, columns_of_piece],
+                ALU.mult,
             )
             var_ps = banks.tile([P, N // NORM_PIECES], FP32, name="var_ps", tag="p_side")
-            nc.tensor.matmul(
-                var_ps[:], mean_weights[:], squared_sum[:, columns_of_piece], start=True, stop=True
-            )
+            for cb in (1, 0):
+                nc.tensor.matmul(
+                    var_ps[:], mean_weights[:], squared[cb][:, columns_of_piece], start=(cb == 1), stop=(cb == 0)
+                )
             nc.scalar.activation(
                 rstd[:, columns_of_piece], var_ps[:], ACT.Abs_reciprocal_sqrt, bias=EPS
             )
 
         xn = [held.tile([P, N], BF16, name=f"xn{cb}") for cb in range(CB)]
-        scaled = [held.tile([P, N], FP32, name=f"scaled{cb}") for cb in range(CB)]
+        scaled = [held.tile([P, N // NORM_PIECES], FP32, name=f"scaled{cb}") for cb in range(CB)]
         for columns_of_piece in piece_columns:
             for cb in range(CB):
                 nc.vector.scalar_tensor_tensor(
-                    scaled[cb][:, columns_of_piece],
+                    scaled[cb][:],
                     centred[cb][:, columns_of_piece],
                     gain_sb[:, cb : cb + 1],
                     rstd[:, columns_of_piece],
@@ -118,12 +114,9 @@ def tile_retnetclm_kernel(tc, base, x, gain, shift, w1, w2, offs, out):
                 )
             for cb in range(CB):
                 nc.vector.tensor_scalar_add(
-                    xn[cb][:, columns_of_piece],
-                    scaled[cb][:, columns_of_piece],
-                    shift_sb[:, cb : cb + 1],
+                    xn[cb][:, columns_of_piece], scaled[cb][:], shift_sb[:, cb : cb + 1]
                 )
 
-        table_choice = held.tile([P, 1], FP32, name="table_choice")
         nc.scalar.activation(table_choice[:], rstd[:, N - 1 : N], ACT.Silu)
 
 
@@ -208,13 +201,15 @@ def tile_retnetclm_kernel(tc, base, x, gain, shift, w1, w2, offs, out):
             half_over_d_ps.append(banks.tile([P, N], FP32, name="half_over_d_ps", tag="q_side"))
             nc.tensor.matmul(half_over_d_ps[fb][:], identity[:], half_over_d[:], start=True, stop=True)
         y_ps = [banks.tile([P, N], FP32, name=f"y_ps{cb}", tag="p_side") for cb in range(CB)]
+        a_re, a_im_neg = [], []
         for fb in range(FB):
-            a_re = work.tile([P, N], BF16, name="a_re")
-            nc.vector.tensor_tensor(a_re[:], num_re[fb][:], half_over_d_ps[fb][:], ALU.mult)
-            a_im_neg = work.tile([P, N], BF16, name="a_im_neg")
-            nc.vector.tensor_tensor(a_im_neg[:], num_im_neg[fb][:], half_over_d_ps[fb][:], ALU.mult)
-            for a_part, w2_block in ((a_re, fb), (a_im_neg, FB + fb)):
-                for cb in range(CB):
+            a_re.append(work.tile([P, N], BF16, name="a_re"))
+            nc.vector.tensor_tensor(a_re[fb][:], num_re[fb][:], half_over_d_ps[fb][:], ALU.mult)
+            a_im_neg.append(work.tile([P, N], BF16, name="a_im_neg"))
+            nc.vector.tensor_tensor(a_im_neg[fb][:], num_im_neg[fb][:], half_over_d_ps[fb][:], ALU.mult)
+        for cb in range(CB):
+            for fb in range(FB):
+                for a_part, w2_block in ((a_re[fb], fb), (a_im_neg[fb], FB + fb)):
                     nc.tensor.matmul(
                         y_ps[cb][:],
                         w2_sb[:, w2_block, cb * P : (cb + 1) * P],

@@ -175,55 +175,88 @@ def tile_retnetclm_kernel(tc, base, x, gain, shift, w1, w2, offs, out):
             a_minus_1.append(work.tile([P, N], FP32, name="a_minus_1"))
             nc.gpsimd.tensor_tensor(a_minus_1[fb][:], tanh_half[fb][:], d_minus_1[fb][:], ALU.add)
 
+        half_over_d = []
+        for fb in range(FB):
+            rsqrt_d = work.tile([P, N], FP32, name="rsqrt_d")
+            nc.scalar.activation(rsqrt_d[:], d_minus_1[fb][:], ACT.Abs_reciprocal_sqrt, bias=1.0)
+            half_over_d.append(work.tile([P, N], FP32, name="half_over_d"))
+            nc.scalar.activation(half_over_d[fb][:], rsqrt_d[:], ACT.Square, scale=math.sqrt(0.5))
+
+        def add_on_tensor(first_product, second_product):
+            total_ps = banks.tile([P, N], FP32, name="total_ps", tag="p_side")
+            nc.tensor.matmul(total_ps[:], identity[:], first_product[:], start=True, stop=False)
+            nc.tensor.matmul(total_ps[:], identity[:], second_product[:], start=False, stop=True)
+            return total_ps
+
         num_re, num_im_neg = [], []
+        a_re = [work.tile([P, N], BF16, name="a_re") for fb in range(FB)]
+        a_im_neg = [work.tile([P, N], BF16, name="a_im_neg") for fb in range(FB)]
         for fb in range(FB):
             q_ps = banks.tile([P, N], FP32, name="q_ps", tag="q_side")
             first_layer(q_ps, F + fb * P, slice(0, N))
             n_p = work.tile([P, N], FP32, name="n_p")
-            nc.vector.scalar_tensor_tensor(n_p[:], n_term[fb][:], 0.5, p_ps[fb][:], ALU.mult, ALU.mult)
+            nc.vector.scalar_tensor_tensor(
+                n_p[:], n_term[fb][:], -0.5 if fb < 2 else 0.5, p_ps[fb][:], ALU.mult, ALU.mult
+            )
             a_p = work.tile([P, N], FP32, name="a_p")
             nc.vector.scalar_tensor_tensor(a_p[:], a_minus_1[fb][:], 1.0, p_ps[fb][:], ALU.add, ALU.mult)
             n_q = work.tile([P, N], FP32, name="n_q")
             nc.vector.scalar_tensor_tensor(n_q[:], n_term[fb][:], 0.5, q_ps[:], ALU.mult, ALU.mult)
-            num_re.append(work.tile([P, N], FP32, name="num_re"))
-            nc.gpsimd.tensor_tensor(num_re[fb][:], a_p[:], n_q[:], ALU.add)
             a_q = work.tile([P, N], FP32, name="a_q")
             nc.vector.scalar_tensor_tensor(a_q[:], a_minus_1[fb][:], 1.0, q_ps[:], ALU.add, ALU.mult)
-            num_im_neg.append(work.tile([P, N], FP32, name="num_im_neg"))
-            nc.gpsimd.tensor_tensor(num_im_neg[fb][:], n_p[:], a_q[:], ALU.subtract)
+            if fb == 0:
+                num_re.append(add_on_tensor(a_p, n_q))
+            else:
+                num_re.append(work.tile([P, N], FP32, name="num_re"))
+                nc.gpsimd.tensor_tensor(num_re[fb][:], a_p[:], n_q[:], ALU.add)
+            if fb == 1:
+                nc.gpsimd.tensor_tensor(a_re[fb][:], num_re[fb][:], half_over_d[fb][:], ALU.mult)
+            if fb < 2:
+                num_im_neg.append(add_on_tensor(n_p, a_q))
+            else:
+                num_im_neg.append(work.tile([P, N], FP32, name="num_im_neg"))
+                nc.gpsimd.tensor_tensor(num_im_neg[fb][:], n_p[:], a_q[:], ALU.subtract)
 
-        half_over_d_ps = []
+        halves = [slice(0, N // 2), slice(N // 2, N)]
+        y_halves_ps = [banks.tile([P, N // 2], FP32, name="y_half_ps", tag="p_side") for half in halves]
+        y_ps = banks.tile([P, N], FP32, name="y_ps", tag="p_side")
         for fb in range(FB):
-            rsqrt_d = work.tile([P, N], FP32, name="rsqrt_d")
-            nc.scalar.activation(rsqrt_d[:], d_minus_1[fb][:], ACT.Abs_reciprocal_sqrt, bias=1.0)
-            half_over_d = work.tile([P, N], FP32, name="half_over_d")
-            nc.scalar.activation(half_over_d[:], rsqrt_d[:], ACT.Square, scale=math.sqrt(0.5))
-            half_over_d_ps.append(banks.tile([P, N], FP32, name="half_over_d_ps", tag="q_side"))
-            nc.tensor.matmul(half_over_d_ps[fb][:], identity[:], half_over_d[:], start=True, stop=True)
-        y_ps = [banks.tile([P, N], FP32, name=f"y_ps{cb}", tag="p_side") for cb in range(CB)]
-        a_re, a_im_neg = [], []
-        for fb in range(FB):
-            a_re.append(work.tile([P, N], BF16, name="a_re"))
-            nc.vector.tensor_tensor(a_re[fb][:], num_re[fb][:], half_over_d_ps[fb][:], ALU.mult)
-            a_im_neg.append(work.tile([P, N], BF16, name="a_im_neg"))
-            nc.vector.tensor_tensor(a_im_neg[fb][:], num_im_neg[fb][:], half_over_d_ps[fb][:], ALU.mult)
+            if fb < 2:
+                if fb == 0:
+                    nc.vector.tensor_tensor(a_re[fb][:], num_re[fb][:], half_over_d[fb][:], ALU.mult)
+                nc.vector.scalar_tensor_tensor(
+                    a_im_neg[fb][:], num_im_neg[fb][:], -1.0, half_over_d[fb][:], ALU.mult, ALU.mult
+                )
+            else:
+                half_over_d_ps = banks.tile([P, N], FP32, name="half_over_d_ps", tag="q_side")
+                nc.tensor.matmul(half_over_d_ps[:], identity[:], half_over_d[fb][:], start=True, stop=True)
+                nc.vector.tensor_tensor(a_re[fb][:], num_re[fb][:], half_over_d_ps[:], ALU.mult)
+                for columns in halves if fb == FB - 1 else [slice(0, N)]:
+                    nc.vector.tensor_tensor(
+                        a_im_neg[fb][:, columns], num_im_neg[fb][:, columns], half_over_d_ps[:, columns], ALU.mult
+                    )
         for cb in range(CB):
-            for fb in range(FB):
-                for a_part, w2_block in ((a_re[fb], fb), (a_im_neg[fb], FB + fb)):
+            feature_blocks = range(FB) if cb == 0 else reversed(range(FB))
+            terms = []
+            for fb in feature_blocks:
+                terms += [(a_re[fb], fb), (a_im_neg[fb], FB + fb)]
+            for step, (a_part, w2_block) in enumerate(terms):
+                for y_part_ps, columns in zip(y_halves_ps, halves) if cb == 0 else [(y_ps, slice(0, N))]:
                     nc.tensor.matmul(
-                        y_ps[cb][:],
+                        y_part_ps[:],
                         w2_sb[:, w2_block, cb * P : (cb + 1) * P],
-                        a_part[:],
-                        start=(w2_block == 0),
-                        stop=(w2_block == 2 * FB - 1),
+                        a_part[:, columns],
+                        start=(step == 0),
+                        stop=(step == len(terms) - 1),
                     )
 
-        copy_of_block = (nc.vector.tensor_copy, nc.scalar.copy)
+        y_sb = [held.tile([P, N], FP32, name=f"y_sb{cb}") for cb in range(CB)]
+        nc.scalar.copy(y_sb[0][:, halves[0]], y_halves_ps[0][:])
+        nc.vector.tensor_copy(y_sb[0][:, halves[1]], y_halves_ps[1][:])
+        nc.scalar.copy(y_sb[1][:], y_ps[:])
         store_queue = (nc.sync, nc.scalar)
         for cb in range(CB):
-            y_sb = held.tile([P, N], FP32, name=f"y_sb{cb}")
-            copy_of_block[cb](y_sb[:], y_ps[cb][:])
             nc.vector.tensor_tensor(
-                window[cb][:].indirect(offsets[:]), y_sb[:], x_sb[cb][:], ALU.add
+                window[cb][:].indirect(offsets[:]), y_sb[cb][:], x_sb[cb][:], ALU.add
             )
             store_queue[cb].dma_start(out[cb * P : (cb + 1) * P, :], window[cb][:])

@@ -133,6 +133,8 @@ def tile_retnetclm_kernel(tc, base, x, gain, shift, w1, w2, offs, out):
         p_ps, turn_part = [], []
         for fb in range(FB):
             q_ps = banks.tile([P, N], FP32, name="q_ps", tag="q_side")
+            if fb == 0:
+                first_q_ps = q_ps
             for columns_of_piece in piece_columns:
                 first_layer(q_ps, F + fb * P, columns_of_piece)
             p_ps.append(banks.tile([P, N], FP32, name="p_ps", tag="p_side"))
@@ -145,7 +147,7 @@ def tile_retnetclm_kernel(tc, base, x, gain, shift, w1, w2, offs, out):
                 turn_part[fb][:], q_ps[:], TURNS_PER_Q, whole_turns[:], ALU.mult, ALU.subtract
             )
 
-        tanh_half, tanh_squared_ps = [], []
+        tanh_half, tanh_squared_in = [], []
         for fb in range(FB):
             tanh_half.append(work.tile([P, N], FP32, name="tanh_half"))
             nc.scalar.activation(tanh_half[fb][:], p_ps[fb][:], ACT.Tanh, scale=ALPHA / 2.0)
@@ -154,8 +156,11 @@ def tile_retnetclm_kernel(tc, base, x, gain, shift, w1, w2, offs, out):
                 nc.gpsimd.tensor_tensor(tanh_squared[:], tanh_half[fb][:], tanh_half[fb][:], ALU.mult)
             else:
                 nc.scalar.activation(tanh_squared[:], tanh_half[fb][:], ACT.Square)
-            tanh_squared_ps.append(banks.tile([P, N], FP32, name="tanh_squared_ps", tag="q_side"))
-            nc.tensor.matmul(tanh_squared_ps[fb][:], identity[:], tanh_squared[:], start=True, stop=True)
+            if fb == 0:
+                tanh_squared_in.append(tanh_squared)
+            else:
+                tanh_squared_in.append(banks.tile([P, N], FP32, name="tanh_squared_ps", tag="q_side"))
+                nc.tensor.matmul(tanh_squared_in[fb][:], identity[:], tanh_squared[:], start=True, stop=True)
         d_minus_1, n_term, a_minus_1 = [], [], []
         for fb in range(FB):
             sine_half = work.tile([P, N], FP32, name="sine_half")
@@ -166,11 +171,11 @@ def tile_retnetclm_kernel(tc, base, x, gain, shift, w1, w2, offs, out):
             nc.scalar.activation(sine_half_squared[:], sine_half[:], ACT.Square)
             d_minus_1.append(work.tile([P, N], FP32, name="d_minus_1"))
             nc.vector.scalar_tensor_tensor(
-                d_minus_1[fb][:], tanh_squared_ps[fb][:], -1.0, sine_half_squared[:], ALU.add, ALU.mult
+                d_minus_1[fb][:], tanh_squared_in[fb][:], -1.0, sine_half_squared[:], ALU.add, ALU.mult
             )
             n_term.append(work.tile([P, N], FP32, name="n_term"))
             nc.vector.scalar_tensor_tensor(
-                n_term[fb][:], tanh_squared_ps[fb][:], -1.0, sine[:], ALU.add, ALU.mult
+                n_term[fb][:], tanh_squared_in[fb][:], -1.0, sine[:], ALU.add, ALU.mult
             )
             a_minus_1.append(work.tile([P, N], FP32, name="a_minus_1"))
             nc.gpsimd.tensor_tensor(a_minus_1[fb][:], tanh_half[fb][:], d_minus_1[fb][:], ALU.add)
@@ -192,8 +197,11 @@ def tile_retnetclm_kernel(tc, base, x, gain, shift, w1, w2, offs, out):
         a_re = [work.tile([P, N], BF16, name="a_re") for fb in range(FB)]
         a_im_neg = [work.tile([P, N], BF16, name="a_im_neg") for fb in range(FB)]
         for fb in range(FB):
-            q_ps = banks.tile([P, N], FP32, name="q_ps", tag="q_side")
-            first_layer(q_ps, F + fb * P, slice(0, N))
+            if fb == 0:
+                q_ps = first_q_ps
+            else:
+                q_ps = banks.tile([P, N], FP32, name="q_ps", tag="q_side")
+                first_layer(q_ps, F + fb * P, slice(0, N))
             n_p = work.tile([P, N], FP32, name="n_p")
             nc.vector.scalar_tensor_tensor(
                 n_p[:], n_term[fb][:], -0.5 if fb < 2 else 0.5, p_ps[fb][:], ALU.mult, ALU.mult

@@ -148,7 +148,8 @@ def tile_retnetclm_kernel(tc, base, x, gain, shift, w1, w2, offs, out):
             )
 
         tanh_half, tanh_squared_in = [], []
-        for fb in range(FB):
+
+        def tangent(fb):
             tanh_half.append(work.tile([P, N], FP32, name="tanh_half"))
             nc.scalar.activation(tanh_half[fb][:], p_ps[fb][:], ACT.Tanh, scale=ALPHA / 2.0)
             tanh_squared = work.tile([P, N], FP32, name="tanh_squared")
@@ -161,8 +162,13 @@ def tile_retnetclm_kernel(tc, base, x, gain, shift, w1, w2, offs, out):
             else:
                 tanh_squared_in.append(banks.tile([P, N], FP32, name="tanh_squared_ps", tag="q_side"))
                 nc.tensor.matmul(tanh_squared_in[fb][:], identity[:], tanh_squared[:], start=True, stop=True)
+
+        for fb in range(FB - 1):
+            tangent(fb)
         d_minus_1, n_term, a_minus_1 = [], [], []
         for fb in range(FB):
+            if fb == 2:
+                tangent(FB - 1)
             sine_half = work.tile([P, N], FP32, name="sine_half")
             nc.scalar.activation(sine_half[:], turn_part[fb][:], ACT.Sin, scale=TWO_PI_BELOW / 2.0)
             sine = work.tile([P, N], FP32, name="sine")
@@ -187,13 +193,7 @@ def tile_retnetclm_kernel(tc, base, x, gain, shift, w1, w2, offs, out):
             half_over_d.append(work.tile([P, N], FP32, name="half_over_d"))
             nc.scalar.activation(half_over_d[fb][:], rsqrt_d[:], ACT.Square, scale=math.sqrt(0.5))
 
-        def add_on_tensor(first_product, second_product):
-            total_ps = banks.tile([P, N], FP32, name="total_ps", tag="p_side")
-            nc.tensor.matmul(total_ps[:], identity[:], first_product[:], start=True, stop=False)
-            nc.tensor.matmul(total_ps[:], identity[:], second_product[:], start=False, stop=True)
-            return total_ps
-
-        num_re, num_im_neg = [], []
+        num_re_ps = []
         a_re = [work.tile([P, N], BF16, name="a_re") for fb in range(FB)]
         a_im_neg = [work.tile([P, N], BF16, name="a_im_neg") for fb in range(FB)]
         for fb in range(FB):
@@ -203,46 +203,31 @@ def tile_retnetclm_kernel(tc, base, x, gain, shift, w1, w2, offs, out):
                 q_ps = banks.tile([P, N], FP32, name="q_ps", tag="q_side")
                 first_layer(q_ps, F + fb * P, slice(0, N))
             n_p = work.tile([P, N], FP32, name="n_p")
-            nc.vector.scalar_tensor_tensor(
-                n_p[:], n_term[fb][:], -0.5 if fb < 2 else 0.5, p_ps[fb][:], ALU.mult, ALU.mult
-            )
+            nc.vector.scalar_tensor_tensor(n_p[:], n_term[fb][:], 0.5, p_ps[fb][:], ALU.mult, ALU.mult)
             a_p = work.tile([P, N], FP32, name="a_p")
             nc.vector.scalar_tensor_tensor(a_p[:], a_minus_1[fb][:], 1.0, p_ps[fb][:], ALU.add, ALU.mult)
             n_q = work.tile([P, N], FP32, name="n_q")
             nc.vector.scalar_tensor_tensor(n_q[:], n_term[fb][:], 0.5, q_ps[:], ALU.mult, ALU.mult)
             a_q = work.tile([P, N], FP32, name="a_q")
             nc.vector.scalar_tensor_tensor(a_q[:], a_minus_1[fb][:], 1.0, q_ps[:], ALU.add, ALU.mult)
-            if fb == 0:
-                num_re.append(add_on_tensor(a_p, n_q))
-            else:
-                num_re.append(work.tile([P, N], FP32, name="num_re"))
-                nc.gpsimd.tensor_tensor(num_re[fb][:], a_p[:], n_q[:], ALU.add)
-            if fb == 1:
-                nc.gpsimd.tensor_tensor(a_re[fb][:], num_re[fb][:], half_over_d[fb][:], ALU.mult)
-            if fb < 2:
-                num_im_neg.append(add_on_tensor(n_p, a_q))
-            else:
-                num_im_neg.append(work.tile([P, N], FP32, name="num_im_neg"))
-                nc.gpsimd.tensor_tensor(num_im_neg[fb][:], n_p[:], a_q[:], ALU.subtract)
+            num_re_ps.append(banks.tile([P, N], FP32, name="num_re_ps", tag="p_side"))
+            nc.tensor.matmul(num_re_ps[fb][:], identity[:], a_p[:], start=True, stop=False)
+            nc.tensor.matmul(num_re_ps[fb][:], identity[:], n_q[:], start=False, stop=True)
+            num_im_neg = work.tile([P, N], FP32, name="num_im_neg")
+            if fb < FB - 1:
+                nc.gpsimd.tensor_tensor(num_im_neg[:], n_p[:], a_q[:], ALU.subtract)
+                nc.gpsimd.tensor_tensor(a_im_neg[fb][:], num_im_neg[:], half_over_d[fb][:], ALU.mult)
 
         halves = [slice(0, N // 2), slice(N // 2, N)]
         y_halves_ps = [banks.tile([P, N // 2], FP32, name="y_half_ps", tag="p_side") for half in halves]
         y_ps = banks.tile([P, N], FP32, name="y_ps", tag="p_side")
         for fb in range(FB):
-            if fb < 2:
-                if fb == 0:
-                    nc.vector.tensor_tensor(a_re[fb][:], num_re[fb][:], half_over_d[fb][:], ALU.mult)
-                nc.vector.scalar_tensor_tensor(
-                    a_im_neg[fb][:], num_im_neg[fb][:], -1.0, half_over_d[fb][:], ALU.mult, ALU.mult
-                )
-            else:
-                half_over_d_ps = banks.tile([P, N], FP32, name="half_over_d_ps", tag="q_side")
-                nc.tensor.matmul(half_over_d_ps[:], identity[:], half_over_d[fb][:], start=True, stop=True)
-                nc.vector.tensor_tensor(a_re[fb][:], num_re[fb][:], half_over_d_ps[:], ALU.mult)
-                for columns in halves if fb == FB - 1 else [slice(0, N)]:
-                    nc.vector.tensor_tensor(
-                        a_im_neg[fb][:, columns], num_im_neg[fb][:, columns], half_over_d_ps[:, columns], ALU.mult
-                    )
+            nc.vector.tensor_tensor(a_re[fb][:], num_re_ps[fb][:], half_over_d[fb][:], ALU.mult)
+        nc.vector.tensor_tensor(num_im_neg[:], n_p[:], a_q[:], ALU.subtract)
+        for columns in halves:
+            nc.vector.tensor_tensor(
+                a_im_neg[FB - 1][:, columns], num_im_neg[:, columns], half_over_d[FB - 1][:, columns], ALU.mult
+            )
         for cb in range(CB):
             feature_blocks = range(FB) if cb == 0 else reversed(range(FB))
             terms = []

@@ -147,7 +147,12 @@ def tile_retnetclm_kernel(tc, base, x, gain, shift, w1, w2, offs, out):
                 turn_part[fb][:], q_ps[:], TURNS_PER_Q, whole_turns[:], ALU.mult, ALU.subtract
             )
 
-        tanh_half, tanh_squared_in = [], []
+        tanh_half, tanh_squared_ps = [], []
+
+        def copy_to_psum(tile):
+            tile_ps = banks.tile([P, N], FP32, name="tile_ps", tag="q_side")
+            nc.tensor.matmul(tile_ps[:], identity[:], tile[:], start=True, stop=True)
+            return tile_ps
 
         def tangent(fb):
             tanh_half.append(work.tile([P, N], FP32, name="tanh_half"))
@@ -157,11 +162,7 @@ def tile_retnetclm_kernel(tc, base, x, gain, shift, w1, w2, offs, out):
                 nc.gpsimd.tensor_tensor(tanh_squared[:], tanh_half[fb][:], tanh_half[fb][:], ALU.mult)
             else:
                 nc.scalar.activation(tanh_squared[:], tanh_half[fb][:], ACT.Square)
-            if fb == 0:
-                tanh_squared_in.append(tanh_squared)
-            else:
-                tanh_squared_in.append(banks.tile([P, N], FP32, name="tanh_squared_ps", tag="q_side"))
-                nc.tensor.matmul(tanh_squared_in[fb][:], identity[:], tanh_squared[:], start=True, stop=True)
+            tanh_squared_ps.append(copy_to_psum(tanh_squared))
 
         for fb in range(FB - 1):
             tangent(fb)
@@ -177,11 +178,11 @@ def tile_retnetclm_kernel(tc, base, x, gain, shift, w1, w2, offs, out):
             nc.scalar.activation(sine_half_squared[:], sine_half[:], ACT.Square)
             d_minus_1.append(work.tile([P, N], FP32, name="d_minus_1"))
             nc.vector.scalar_tensor_tensor(
-                d_minus_1[fb][:], tanh_squared_in[fb][:], -1.0, sine_half_squared[:], ALU.add, ALU.mult
+                d_minus_1[fb][:], tanh_squared_ps[fb][:], -1.0, sine_half_squared[:], ALU.add, ALU.mult
             )
             n_term.append(work.tile([P, N], FP32, name="n_term"))
             nc.vector.scalar_tensor_tensor(
-                n_term[fb][:], tanh_squared_in[fb][:], -1.0, sine[:], ALU.add, ALU.mult
+                n_term[fb][:], tanh_squared_ps[fb][:], -1.0, sine[:], ALU.add, ALU.mult
             )
             a_minus_1.append(work.tile([P, N], FP32, name="a_minus_1"))
             nc.gpsimd.tensor_tensor(a_minus_1[fb][:], tanh_half[fb][:], d_minus_1[fb][:], ALU.add)
@@ -204,6 +205,8 @@ def tile_retnetclm_kernel(tc, base, x, gain, shift, w1, w2, offs, out):
                 first_layer(q_ps, F + fb * P, slice(0, N))
             n_p = work.tile([P, N], FP32, name="n_p")
             nc.vector.scalar_tensor_tensor(n_p[:], n_term[fb][:], 0.5, p_ps[fb][:], ALU.mult, ALU.mult)
+            if fb == FB - 1:
+                n_p_ps = copy_to_psum(n_p)
             a_p = work.tile([P, N], FP32, name="a_p")
             nc.vector.scalar_tensor_tensor(a_p[:], a_minus_1[fb][:], 1.0, p_ps[fb][:], ALU.add, ALU.mult)
             n_q = work.tile([P, N], FP32, name="n_q")
@@ -223,10 +226,11 @@ def tile_retnetclm_kernel(tc, base, x, gain, shift, w1, w2, offs, out):
         y_ps = banks.tile([P, N], FP32, name="y_ps", tag="p_side")
         for fb in range(FB):
             nc.vector.tensor_tensor(a_re[fb][:], num_re_ps[fb][:], half_over_d[fb][:], ALU.mult)
-        nc.vector.tensor_tensor(num_im_neg[:], n_p[:], a_q[:], ALU.subtract)
+        half_over_d_ps = copy_to_psum(half_over_d[FB - 1])
+        nc.vector.tensor_tensor(num_im_neg[:], n_p_ps[:], a_q[:], ALU.subtract)
         for columns in halves:
             nc.vector.tensor_tensor(
-                a_im_neg[FB - 1][:, columns], num_im_neg[:, columns], half_over_d[FB - 1][:, columns], ALU.mult
+                a_im_neg[FB - 1][:, columns], num_im_neg[:, columns], half_over_d_ps[:, columns], ALU.mult
             )
         for cb in range(CB):
             feature_blocks = range(FB) if cb == 0 else reversed(range(FB))

@@ -205,8 +205,6 @@ def tile_retnetclm_kernel(tc, base, x, gain, shift, w1, w2, offs, out):
                 first_layer(q_ps, F + fb * P, slice(0, N))
             n_p = work.tile([P, N], FP32, name="n_p")
             nc.vector.scalar_tensor_tensor(n_p[:], n_term[fb][:], 0.5, p_ps[fb][:], ALU.mult, ALU.mult)
-            if fb == FB - 1:
-                n_p_ps = copy_to_psum(n_p)
             a_p = work.tile([P, N], FP32, name="a_p")
             nc.vector.scalar_tensor_tensor(a_p[:], a_minus_1[fb][:], 1.0, p_ps[fb][:], ALU.add, ALU.mult)
             n_q = work.tile([P, N], FP32, name="n_q")
@@ -226,11 +224,10 @@ def tile_retnetclm_kernel(tc, base, x, gain, shift, w1, w2, offs, out):
         y_ps = banks.tile([P, N], FP32, name="y_ps", tag="p_side")
         for fb in range(FB):
             nc.vector.tensor_tensor(a_re[fb][:], num_re_ps[fb][:], half_over_d[fb][:], ALU.mult)
-        half_over_d_ps = copy_to_psum(half_over_d[FB - 1])
-        nc.vector.tensor_tensor(num_im_neg[:], n_p_ps[:], a_q[:], ALU.subtract)
+        nc.vector.tensor_tensor(num_im_neg[:], n_p[:], a_q[:], ALU.subtract)
         for columns in halves:
             nc.vector.tensor_tensor(
-                a_im_neg[FB - 1][:, columns], num_im_neg[:, columns], half_over_d_ps[:, columns], ALU.mult
+                a_im_neg[FB - 1][:, columns], num_im_neg[:, columns], half_over_d[FB - 1][:, columns], ALU.mult
             )
         for cb in range(CB):
             feature_blocks = range(FB) if cb == 0 else reversed(range(FB))

import math

import concourse.mybir as mybir
from concourse.masks import make_identity

FP32 = mybir.dt.float32
BF16 = mybir.dt.bfloat16
U16 = mybir.dt.uint16
I32 = mybir.dt.int32
ALU = mybir.AluOpType
ACT = mybir.ActivationFunctionType

P = 128
C, F, S, N = 256, 512, 2048, 512
CB = C // P
FB = F // P
NORM_PIECES = 2
EPS = 1e-8
ALPHA = 1.702

FLOPS = 2 * C * (2 * F) * N + 2 * (2 * F) * C * N

TURNS_PER_Q = ALPHA / (2.0 * math.pi)
TWO_PI_BELOW = 6.2831850051879883


def tile_retnetclm_kernel(tc, base, x, gain, shift, w1, w2, offs, out):
    nc = tc.nc
    with (
        tc.tile_pool(name="held", bufs=1) as held,
        tc.tile_pool(name="work", bufs=FB) as work,
        tc.psum_pool(name="banks", bufs=4) as banks,
    ):
        piece_columns = [
            slice(piece * (N // NORM_PIECES), (piece + 1) * (N // NORM_PIECES))
            for piece in range(NORM_PIECES)
        ]
        x_sb = [held.tile([P, N], FP32, name=f"x_sb{cb}") for cb in range(CB)]
        for columns_of_piece in piece_columns:
            nc.sync.dma_start(x_sb[0][:, columns_of_piece], x[0:P, columns_of_piece])
            nc.scalar.dma_start(x_sb[1][:, columns_of_piece], x[P : 2 * P, columns_of_piece])

        w1_sb = [held.tile([P, 2 * F], BF16, name=f"w1_sb{cb}") for cb in range(CB)]
        nc.sync.dma_start(w1_sb[0][:], w1[0:P, :])
        nc.scalar.dma_start(w1_sb[1][:], w1[P : 2 * P, :])

        offsets = held.tile([P, N // 16], U16, name="offsets")
        nc.sync.dma_start(offsets[:], offs)

        gain_sb = held.tile([P, CB], FP32, name="gain_sb")
        nc.sync.dma_start(gain_sb[:], gain.rearrange("(b p) o -> p (b o)", p=P))
        shift_sb = held.tile([P, CB], FP32, name="shift_sb")
        nc.scalar.dma_start(shift_sb[:], shift.rearrange("(b p) o -> p (b o)", p=P))

        w2_sb = held.tile([P, 2 * FB, C], BF16, name="w2_sb")
        nc.sync.dma_start(w2_sb[:], w2.rearrange("(k p) c -> p k c", p=P))

        window = [held.tile([P, S], FP32, name=f"window{cb}") for cb in range(CB)]
        nc.sync.dma_start(window[0][:], base[0:P, :])
        nc.scalar.dma_start(window[1][:], base[P : 2 * P, :])

        mean_weights = held.tile([P, P], FP32, name="mean_weights")
        nc.vector.memset(mean_weights[:], 1.0 / C)
        identity = held.tile([P, P], FP32, name="identity")
        make_identity(nc, identity[:])
        table_choice = held.tile([P, 1], FP32, name="table_choice")
        nc.scalar.activation(table_choice[:], mean_weights[:, 0:1], ACT.Abs_reciprocal_sqrt)

        x_sum = held.tile([P, N], FP32, name="x_sum")
        mean_ps = []
        for columns_of_piece in piece_columns:
            nc.vector.tensor_tensor(
                x_sum[:, columns_of_piece], x_sb[0][:, columns_of_piece], x_sb[1][:, columns_of_piece], ALU.add
            )
            mean_ps.append(banks.tile([P, N // NORM_PIECES], FP32, name="mean_ps", tag="q_side"))
            nc.tensor.matmul(
                mean_ps[-1][:], mean_weights[:], x_sum[:, columns_of_piece], start=True, stop=True
            )
        centred = [held.tile([P, N], FP32, name=f"centred{cb}") for cb in range(CB)]
        squared = [held.tile([P, N], FP32, name=f"squared{cb}") for cb in range(CB)]
        rstd = held.tile([P, N], FP32, name="rstd")
        for piece, columns_of_piece in enumerate(piece_columns):
            for cb in (1, 0):
                nc.vector.tensor_tensor(
                    centred[cb][:, columns_of_piece], x_sb[cb][:, columns_of_piece], mean_ps[piece][:], ALU.subtract
                )
            nc.scalar.activation(squared[1][:, columns_of_piece], centred[1][:, columns_of_piece], ACT.Square)
            nc.vector.tensor_tensor(
                squared[0][:, columns_of_piece],
                centred[0][:, columns_of_piece],
                centred[0][:, columns_of_piece],
                ALU.mult,
            )
            var_ps = banks.tile([P, N // NORM_PIECES], FP32, name="var_ps", tag="p_side")
            for cb in (1, 0):
                nc.tensor.matmul(
                    var_ps[:], mean_weights[:], squared[cb][:, columns_of_piece], start=(cb == 1), stop=(cb == 0)
                )
            nc.scalar.activation(
                rstd[:, columns_of_piece], var_ps[:], ACT.Abs_reciprocal_sqrt, bias=EPS
            )

        xn = [held.tile([P, N], BF16, name=f"xn{cb}") for cb in range(CB)]
        scaled = [held.tile([P, N // NORM_PIECES], FP32, name=f"scaled{cb}") for cb in range(CB)]
        for columns_of_piece in piece_columns:
            for cb in range(CB):
                nc.vector.scalar_tensor_tensor(
                    scaled[cb][:],
                    centred[cb][:, columns_of_piece],
                    gain_sb[:, cb : cb + 1],
                    rstd[:, columns_of_piece],
                    ALU.mult,
                    ALU.mult,
                )
            for cb in range(CB):
                nc.vector.tensor_scalar_add(
                    xn[cb][:, columns_of_piece], scaled[cb][:], shift_sb[:, cb : cb + 1]
                )

        nc.scalar.activation(table_choice[:], rstd[:, N - 1 : N], ACT.Silu)


        def first_layer(h_ps, first_column, token_columns):
            for cb in range(CB):
                nc.tensor.matmul(
                    h_ps[:, token_columns],
                    w1_sb[cb][:, first_column : first_column + P],
                    xn[cb][:, token_columns],
                    start=(cb == 0),
                    stop=(cb == CB - 1),
                )

        p_ps, turn_part = [], []
        for fb in range(FB):
            q_ps = banks.tile([P, N], FP32, name="q_ps", tag="q_side")
            if fb == 0:
                first_q_ps = q_ps
            for columns_of_piece in piece_columns:
                first_layer(q_ps, F + fb * P, columns_of_piece)
            p_ps.append(banks.tile([P, N], FP32, name="p_ps", tag="p_side"))
            for columns_of_piece in piece_columns:
                first_layer(p_ps[fb], fb * P, columns_of_piece)
            whole_turns = work.tile([P, N], I32, name="whole_turns")
            nc.vector.tensor_scalar(whole_turns[:], q_ps[:], TURNS_PER_Q, None, ALU.mult)
            turn_part.append(work.tile([P, N], FP32, name="turn_part"))
            nc.vector.scalar_tensor_tensor(
                turn_part[fb][:], q_ps[:], TURNS_PER_Q, whole_turns[:], ALU.mult, ALU.subtract
            )

        tanh_half, tanh_squared_ps = [], []

        def copy_to_psum(tile):
            tile_ps = banks.tile([P, N], FP32, name="tile_ps", tag="q_side")
            nc.tensor.matmul(tile_ps[:], identity[:], tile[:], start=True, stop=True)
            return tile_ps

        def tangent(fb):
            tanh_half.append(work.tile([P, N], FP32, name="tanh_half"))
            nc.scalar.activation(tanh_half[fb][:], p_ps[fb][:], ACT.Tanh, scale=ALPHA / 2.0)
            tanh_squared = work.tile([P, N], FP32, name="tanh_squared")
            if fb < FB - 1:
                nc.gpsimd.tensor_tensor(tanh_squared[:], tanh_half[fb][:], tanh_half[fb][:], ALU.mult)
            else:
                nc.scalar.activation(tanh_squared[:], tanh_half[fb][:], ACT.Square)
            tanh_squared_ps.append(copy_to_psum(tanh_squared))

        for fb in range(FB - 1):
            tangent(fb)
        d_minus_1, n_term, a_minus_1 = [], [], []
        for fb in range(FB):
            if fb == 2:
                tangent(FB - 1)
            sine_half = work.tile([P, N], FP32, name="sine_half")
            nc.scalar.activation(sine_half[:], turn_part[fb][:], ACT.Sin, scale=TWO_PI_BELOW / 2.0)
            sine = work.tile([P, N], FP32, name="sine")
            nc.scalar.activation(sine[:], turn_part[fb][:], ACT.Sin, scale=TWO_PI_BELOW)
            sine_half_squared = work.tile([P, N], FP32, name="sine_half_squared")
            nc.scalar.activation(sine_half_squared[:], sine_half[:], ACT.Square)
            d_minus_1.append(work.tile([P, N], FP32, name="d_minus_1"))
            nc.vector.scalar_tensor_tensor(
                d_minus_1[fb][:], tanh_squared_ps[fb][:], -1.0, sine_half_squared[:], ALU.add, ALU.mult
            )
            n_term.append(work.tile([P, N], FP32, name="n_term"))
            nc.vector.scalar_tensor_tensor(
                n_term[fb][:], tanh_squared_ps[fb][:], -1.0, sine[:], ALU.add, ALU.mult
            )
            a_minus_1.append(work.tile([P, N], FP32, name="a_minus_1"))
            nc.gpsimd.tensor_tensor(a_minus_1[fb][:], tanh_half[fb][:], d_minus_1[fb][:], ALU.add)

        half_over_d = []
        for fb in range(FB):
            rsqrt_d = work.tile([P, N], FP32, name="rsqrt_d")
            nc.scalar.activation(rsqrt_d[:], d_minus_1[fb][:], ACT.Abs_reciprocal_sqrt, bias=1.0)
            half_over_d.append(work.tile([P, N], FP32, name="half_over_d"))
            nc.scalar.activation(half_over_d[fb][:], rsqrt_d[:], ACT.Square, scale=math.sqrt(0.5))

        num_re_ps = []
        a_re = [work.tile([P, N], BF16, name="a_re") for fb in range(FB)]
        a_im_neg = [work.tile([P, N], BF16, name="a_im_neg") for fb in range(FB)]
        for fb in range(FB):
            if fb == 0:
                q_ps = first_q_ps
            else:
                q_ps = banks.tile([P, N], FP32, name="q_ps", tag="q_side")
                first_layer(q_ps, F + fb * P, slice(0, N))
            n_p = work.tile([P, N], FP32, name="n_p")
            nc.vector.scalar_tensor_tensor(n_p[:], n_term[fb][:], 0.5, p_ps[fb][:], ALU.mult, ALU.mult)
            a_p = work.tile([P, N], FP32, name="a_p")
            nc.vector.scalar_tensor_tensor(a_p[:], a_minus_1[fb][:], 1.0, p_ps[fb][:], ALU.add, ALU.mult)
            n_q = work.tile([P, N], FP32, name="n_q")
            nc.vector.scalar_tensor_tensor(n_q[:], n_term[fb][:], 0.5, q_ps[:], ALU.mult, ALU.mult)
            a_q = work.tile([P, N], FP32, name="a_q")
            nc.vector.scalar_tensor_tensor(a_q[:], a_minus_1[fb][:], 1.0, q_ps[:], ALU.add, ALU.mult)
            num_re_ps.append(banks.tile([P, N], FP32, name="num_re_ps", tag="p_side"))
            nc.tensor.matmul(num_re_ps[fb][:], identity[:], a_p[:], start=True, stop=False)
            nc.tensor.matmul(num_re_ps[fb][:], identity[:], n_q[:], start=False, stop=True)
            num_im_neg = work.tile([P, N], FP32, name="num_im_neg")
            if fb < FB - 1:
                nc.gpsimd.tensor_tensor(num_im_neg[:], n_p[:], a_q[:], ALU.subtract)
                nc.gpsimd.tensor_tensor(a_im_neg[fb][:], num_im_neg[:], half_over_d[fb][:], ALU.mult)

        halves = [slice(0, N // 2), slice(N // 2, N)]
        y_halves_ps = [banks.tile([P, N // 2], FP32, name="y_half_ps", tag="p_side") for half in halves]
        y_ps = banks.tile([P, N], FP32, name="y_ps", tag="p_side")
        for fb in range(FB):
            nc.vector.tensor_tensor(a_re[fb][:], num_re_ps[fb][:], half_over_d[fb][:], ALU.mult)
        nc.vector.tensor_tensor(num_im_neg[:], n_p[:], a_q[:], ALU.subtract)
        for columns in halves:
            nc.vector.tensor_tensor(
                a_im_neg[FB - 1][:, columns], num_im_neg[:, columns], half_over_d[FB - 1][:, columns], ALU.mult
            )
        for cb in range(CB):
            feature_blocks = range(FB) if cb == 0 else reversed(range(FB))
            terms = []
            for fb in feature_blocks:
                terms += [(a_re[fb], fb), (a_im_neg[fb], FB + fb)]
            for step, (a_part, w2_block) in enumerate(terms):
                for y_part_ps, columns in zip(y_halves_ps, halves) if cb == 0 else [(y_ps, slice(0, N))]:
                    nc.tensor.matmul(
                        y_part_ps[:],
                        w2_sb[:, w2_block, cb * P : (cb + 1) * P],
                        a_part[:, columns],
                        start=(step == 0),
                        stop=(step == len(terms) - 1),
                    )

        y_sb = [held.tile([P, N], FP32, name=f"y_sb{cb}") for cb in range(CB)]
        nc.scalar.copy(y_sb[0][:, halves[0]], y_halves_ps[0][:])
        nc.vector.tensor_copy(y_sb[0][:, halves[1]], y_halves_ps[1][:])
        nc.scalar.copy(y_sb[1][:], y_ps[:])
        store_queue = (nc.sync, nc.scalar)
        for cb in range(CB):
            nc.vector.tensor_tensor(
                window[cb][:].indirect(offsets[:]), y_sb[cb][:], x_sb[cb][:], ALU.add
            )
            store_queue[cb].dma_start(out[cb * P : (cb + 1) * P, :], window[cb][:])
